import numpy as np
import ml_dtypes


def mxq(x, axis, fmt="e4m3"):
    dtype, down = {"e4m3": (ml_dtypes.float8_e4m3fn, 7), "e5m2": (ml_dtypes.float8_e5m2, 14)}[fmt]
    v = np.moveaxis(np.asarray(x, np.float32).astype(ml_dtypes.bfloat16).astype(np.float64), axis, -1)
    blocks = v.reshape(v.shape[:-1] + (-1, 32))
    amax = np.abs(blocks).max(-1, keepdims=True)
    byte = np.maximum(np.where(amax > 0, np.frexp(amax)[1] - 1 + 127, 0) - down, 1)
    scale = np.exp2(byte - 127.0)
    codes = (blocks / scale).astype(np.float32).astype(dtype).astype(np.float64)
    return np.moveaxis((codes * scale).reshape(v.shape), -1, axis)


WIDE = False


def mx_kscale(k):
    if not WIDE:
        return np.ones(k)
    levels = np.array([10, -10, 5, -5, 0])
    a = np.random.permutation(np.resize(levels, k // 512 * 4)).reshape(k // 512, 4)
    idx = np.arange(k)
    return np.exp2(a[idx // 512, idx % 128 // 32])


BF16 = ml_dtypes.bfloat16


def bf(x):
    return np.asarray(x, np.float32).astype(BF16)


def f64(x):
    return np.asarray(x).astype(np.float64)


B, S, D, H, HD = 1, 1024, 1024, 4, 512
I = H * HD


def silu(v):
    return v / (1.0 + np.exp(-v))


def setup_inputs():
    t = mx_kscale(I)
    h = silu(np.random.standard_normal((B, S, I))) * np.random.standard_normal((B, S, I))
    return {"h_inter": bf(h * t),
            "adjacency": bf(np.random.uniform(size=(B, H, S, S)) * 2.0 / np.sqrt(S)),
            "Wd": bf(np.random.standard_normal((I, D)) / np.sqrt(I) / t[:, None]),
            "eps": bf(np.random.standard_normal(H) * 0.2),
            "alpha": bf(1.0 + np.random.standard_normal(H) * 0.2)}


def reference(h_inter, adjacency, Wd, eps, alpha):
    h_heads = f64(h_inter).reshape(B, S, H, HD).transpose(0, 2, 1, 3)
    agg = mxq(f64(adjacency), 3, "e4m3") @ mxq(h_heads, 2, "e4m3")
    e = (1.0 + f64(eps))[None, :, None, None]
    a = f64(alpha)[None, :, None, None]
    h_gin = e * h_heads + a * agg
    h_comb = h_gin.transpose(0, 2, 1, 3).reshape(B, S, I)
    return mxq(h_comb, 2, "e4m3") @ mxq(f64(Wd), 0, "e4m3")

@@ -1,0 +1,222 @@
+from contextlib import ExitStack
+
+import concourse.mybir as mybir
+from concourse.masks import make_identity
+
+F32 = mybir.dt.float32
+BF16 = mybir.dt.bfloat16
+U32 = mybir.dt.uint32
+U8 = mybir.dt.uint8
+FP8X4 = mybir.dt.float8_e4m3fn_x4
+ALU = mybir.AluOpType
+ACT = mybir.ActivationFunctionType
+
+P = 128
+PACK = 4
+K_PASS = P * PACK
+S = 1024
+HEADS = 4
+HD = 512
+D = 1024
+BLOCKS = S // K_PASS
+N_HALF = 512
+
+FLOPS = 2 * HEADS * S * S * HD + 2 * S * HEADS * HD * D
+
+
+def tile_llamamlp_halfwaygin_pa_kernel(tc, h_inter, adjacency, Wd, eps, alpha, out):
+    nc = tc.nc
+
+    h_view = h_inter.rearrange("b (c u p e) f -> (b c) u p e f", c=BLOCKS, u=2, p=P, e=2)
+    a_view = adjacency.rearrange("b n (c u p e) j -> (b n) c p u (e j)", c=BLOCKS, u=2, p=P, e=2)
+    wd_view = Wd.rearrange("(n u p e) d -> n p u (e d)", n=HEADS, u=2, p=P, e=2)
+    out_view = out.rearrange("b (c u p e) d -> (b c) u p e d", c=BLOCKS, u=2, p=P, e=2)
+
+    with ExitStack() as ctx:
+        keep = ctx.enter_context(tc.tile_pool(name="keep", bufs=1))
+        raw = ctx.enter_context(tc.tile_pool(name="raw", bufs=4))
+        work = ctx.enter_context(tc.tile_pool(name="work", bufs=2))
+        psum_tr = ctx.enter_context(tc.psum_pool(name="psum_tr", bufs=4))
+        psum_acc = ctx.enter_context(tc.psum_pool(name="psum_acc", bufs=4))
+
+        ident = keep.tile([P, P], F32, name="ident")
+        make_identity(nc, ident[:])
+        eps_bf = keep.tile([P, HEADS], BF16, name="eps_bf")
+        alpha_bf = keep.tile([P, HEADS], BF16, name="alpha_bf")
+        nc.scalar.dma_start(out=eps_bf[:], in_=eps.partition_broadcast(P))
+        nc.scalar.dma_start(out=alpha_bf[:], in_=alpha.partition_broadcast(P))
+        one_plus_eps = keep.tile([P, HEADS], F32, name="one_plus_eps")
+        alpha_f = keep.tile([P, HEADS], F32, name="alpha_f")
+        nc.vector.tensor_scalar_add(out=one_plus_eps[:], in0=eps_bf[:], scalar1=1.0)
+        nc.vector.tensor_copy(out=alpha_f[:], in_=alpha_bf[:])
+
+        h_raw = [keep.tile([P, BLOCKS, PACK, HD], BF16, name="h_raw%d" % n) for n in range(HEADS)]
+        wd_raw = [keep.tile([P, PACK, D], BF16, name="wd_raw%d" % n) for n in range(HEADS)]
+        h_codes = keep.tile([P, BLOCKS, HEADS, HD], U32, name="h_codes", align_bytes=64)
+        h_scales = keep.tile([P, BLOCKS, HEADS, HD], U8, name="h_scales", align_bytes=64)
+        wd_codes = keep.tile([P, HEADS, D], U32, name="wd_codes", align_bytes=64)
+        wd_scales = keep.tile([P, HEADS, D], U8, name="wd_scales", align_bytes=64)
+        g_codes = keep.tile([P, HEADS, BLOCKS, K_PASS], U32, name="g_codes", align_bytes=64)
+        g_scales = keep.tile([P, HEADS, BLOCKS, K_PASS], U8, name="g_scales", align_bytes=64)
+
+        a_raw = {}
+        a_codes = {}
+        a_scales = {}
+        h_scaled = {}
+
+        def load_unit(c, n):
+            if c == 0:
+                for cc in range(BLOCKS):
+                    for u in range(2):
+                        nc.sync.dma_start(
+                            out=h_raw[n][:, cc, 2 * u : 2 * u + 2, :],
+                            in_=h_view[cc, u, :, :, HD * n : HD * (n + 1)],
+                        )
+            a_raw[(c, n)] = raw.tile([P, PACK, S], BF16, name="a_raw")
+            nc.sync.dma_start(
+                out=a_raw[(c, n)][:].rearrange("p (u e) j -> p u (e j)", u=2),
+                in_=a_view[n, c, :, :, :],
+            )
+            if c == 1:
+                nc.sync.dma_start(
+                    out=wd_raw[n][:].rearrange("p (u e) d -> p u (e d)", u=2),
+                    in_=wd_view[n, :, :, :],
+                )
+
+        def quantise_h(n):
+            for cc in range(BLOCKS):
+                h_grouped = work.tile([P, HD, PACK], BF16, tag="grouped", bufs=3, align_bytes=64)
+                dst = h_grouped[:].rearrange("p (u e q) t -> p e u q t", u=2, e=2)
+                src = h_raw[n][:, cc, :, :].rearrange("p t (u q e) -> p e u q t", u=2, e=2)
+                nc.vector.tensor_copy(out=dst[:, 0, :, :, :], in_=src[:, 0, :, :, :])
+                nc.scalar.copy(out=dst[:, 1, :, :, :], in_=src[:, 1, :, :, :])
+                nc.vector.quantize_mx(
+                    out=h_codes[:, cc, n, :].bitcast(FP8X4),
+                    scales=h_scales[:, cc, n, :],
+                    in_=h_grouped[:].rearrange("p x t -> p (x t)"),
+                )
+
+        def quantise_wd(n):
+            for dh in range(D // N_HALF):
+                cols = slice(N_HALF * dh, N_HALF * (dh + 1))
+                wd_grouped = work.tile([P, N_HALF, PACK], BF16, tag="grouped", bufs=3, align_bytes=64)
+                nc.vector.tensor_copy(
+                    out=wd_grouped[:].rearrange("p (x i) t -> p x t i", i=4),
+                    in_=wd_raw[n][:, :, cols].rearrange("p t (x i) -> p x t i", i=4),
+                )
+                nc.vector.quantize_mx(
+                    out=wd_codes[:, n, cols].bitcast(FP8X4),
+                    scales=wd_scales[:, n, cols],
+                    in_=wd_grouped[:].rearrange("p x t -> p (x t)"),
+                )
+
+        def front(c, n):
+            a_codes[(c, n)] = work.tile([P, PACK, 2 * P], U32, name="a_codes", align_bytes=64)
+            a_scales[(c, n)] = work.tile([P, PACK, 2 * P], U8, name="a_scales", align_bytes=64)
+            for ti in range(PACK):
+                a_words = a_raw[(c, n)][:, ti, :].bitcast(F32)
+                at_ps = psum_tr.tile([P, BLOCKS, 2, P], F32, tag="tr")
+                for cp in range(BLOCKS):
+                    for up in range(2):
+                        w0 = 256 * cp + P * up
+                        nc.tensor.transpose(at_ps[:, cp, up, :], a_words[:, w0 : w0 + P], ident[:])
+                a_grouped = work.tile([P, BLOCKS, P, PACK], BF16, bufs=4, align_bytes=64)
+                nc.scalar.copy(
+                    out=a_grouped[:].bitcast(F32),
+                    in_=at_ps[:].rearrange("p c u i -> p c i u"),
+                )
+                nc.vector.quantize_mx(
+                    out=a_codes[(c, n)][:, ti, :].bitcast(FP8X4),
+                    scales=a_scales[(c, n)][:, ti, :],
+                    in_=a_grouped[:].rearrange("p c i t -> p (c i t)"),
+                )
+            h_scaled[(c, n)] = work.tile([P, PACK * P, PACK], F32, name="h_scaled")
+            for pair in range(2):
+                ht_ps = psum_tr.tile([P, 2, 2 * P], F32, tag="tr")
+                for ti2 in range(2):
+                    h_words = h_raw[n][:, c, 2 * pair + ti2, :].bitcast(F32)
+                    for uf in range(2):
+                        nc.tensor.transpose(
+                            ht_ps[:, uf, P * ti2 : P * (ti2 + 1)],
+                            h_words[:, P * uf : P * (uf + 1)],
+                            ident[:],
+                        )
+                nc.scalar.activation(
+                    out=h_scaled[(c, n)][:, 2 * P * pair : 2 * P * (pair + 1), :].rearrange(
+                        "p x (u e) -> p x u e", e=2
+                    ),
+                    in_=ht_ps[:].bitcast(BF16).rearrange("p u (x e) -> p x u e", e=2),
+                    func=ACT.Copy,
+                    scale=one_plus_eps[:, n : n + 1],
+                )
+
+        def back(c, n):
+            g_grouped = work.tile([P, PACK * P, PACK], BF16, align_bytes=64)
+            for ti in range(PACK):
+                agg_ps = psum_acc.tile([P, PACK, P], F32, tag="acc")
+                for tf in range(PACK):
+                    for cp in range(BLOCKS):
+                        nc.tensor.matmul_mx(
+                            out=agg_ps[:, tf, :],
+                            lhsT=h_codes[:, cp, n, P * tf : P * (tf + 1)].bitcast(FP8X4),
+                            lhsT_scale=h_scales[:, cp, n, P * tf : P * (tf + 1)],
+                            rhs=a_codes[(c, n)][:, ti, P * cp : P * (cp + 1)].bitcast(FP8X4),
+                            rhs_scale=a_scales[(c, n)][:, ti, P * cp : P * (cp + 1)],
+                            start=(cp == 0),
+                            stop=(cp == BLOCKS - 1),
+                        )
+                nc.vector.scalar_tensor_tensor(
+                    out=g_grouped[:, P * ti : P * (ti + 1), :],
+                    in0=agg_ps[:].rearrange("p t i -> p i t"),
+                    scalar=alpha_f[:, n : n + 1],
+                    in1=h_scaled[(c, n)][:, P * ti : P * (ti + 1), :],
+                    op0=ALU.mult,
+                    op1=ALU.add,
+                )
+            nc.vector.quantize_mx(
+                out=g_codes[:, n, c, :].bitcast(FP8X4),
+                scales=g_scales[:, n, c, :],
+                in_=g_grouped[:].rearrange("p x t -> p (x t)"),
+            )
+
+        def down_projection(c):
+            for ti in range(PACK):
+                out_sb = work.tile([P, D], F32, bufs=3)
+                for dh in range(D // N_HALF):
+                    cols = slice(N_HALF * dh, N_HALF * (dh + 1))
+                    out_ps = psum_acc.tile([P, N_HALF], F32, tag="acc")
+                    for n in range(HEADS):
+                        nc.tensor.matmul_mx(
+                            out=out_ps[:],
+                            lhsT=g_codes[:, n, c, P * ti : P * (ti + 1)].bitcast(FP8X4),
+                            lhsT_scale=g_scales[:, n, c, P * ti : P * (ti + 1)],
+                            rhs=wd_codes[:, n, cols].bitcast(FP8X4),
+                            rhs_scale=wd_scales[:, n, cols],
+                            start=(n == 0),
+                            stop=(n == HEADS - 1),
+                        )
+                    if dh == 0:
+                        nc.scalar.copy(out=out_sb[:, cols], in_=out_ps[:])
+                    else:
+                        nc.vector.tensor_copy(out=out_sb[:, cols], in_=out_ps[:])
+                nc.sync.dma_start(out=out_view[c, ti // 2, :, ti % 2, :], in_=out_sb[:])
+
+        units = [(c, n) for c in range(BLOCKS) for n in range(HEADS)]
+        ahead = 4
+        for k in range(ahead):
+            load_unit(*units[k])
+        quantise_h(0)
+        front(*units[0])
+        for k in range(len(units)):
+            c, n = units[k]
+            if k + ahead < len(units):
+                load_unit(*units[k + ahead])
+            if k + 1 < len(units):
+                if units[k + 1][0] == 0:
+                    quantise_h(units[k + 1][1])
+                front(*units[k + 1])
+            back(c, n)
+            if c == 1:
+                quantise_wd(n)
+        for c in range(BLOCKS):
+            down_projection(c)

@@ -19,7 +19,9 @@ HEADS = 4
 HD = 512
 D = 1024
 BLOCKS = S // K_PASS
-N_HALF = 512
+CHUNK = 256
+CHUNKS = D // CHUNK
+A_BUFS = 4
 
 FLOPS = 2 * HEADS * S * S * HD + 2 * S * HEADS * HD * D
 
@@ -32,12 +34,14 @@ def tile_llamamlp_halfwaygin_pa_kernel(tc, h_inter, adjacency, Wd, eps, alpha, o
     wd_view = Wd.rearrange("(n u p e) d -> n p u (e d)", n=HEADS, u=2, p=P, e=2)
     out_view = out.rearrange("b (c u p e) d -> (b c) u p e d", c=BLOCKS, u=2, p=P, e=2)
 
+    units = [(c, n) for c in range(BLOCKS) for n in range(HEADS)]
+
     with ExitStack() as ctx:
         keep = ctx.enter_context(tc.tile_pool(name="keep", bufs=1))
-        raw = ctx.enter_context(tc.tile_pool(name="raw", bufs=4))
         work = ctx.enter_context(tc.tile_pool(name="work", bufs=2))
         psum_tr = ctx.enter_context(tc.psum_pool(name="psum_tr", bufs=4))
         psum_acc = ctx.enter_context(tc.psum_pool(name="psum_acc", bufs=4))
+        ctx.enter_context(tc.manual_schedule())
 
         ident = keep.tile([P, P], F32, name="ident")
         make_identity(nc, ident[:])
@@ -52,116 +56,127 @@ def tile_llamamlp_halfwaygin_pa_kernel(tc, h_inter, adjacency, Wd, eps, alpha, o
 
         h_raw = [keep.tile([P, BLOCKS, PACK, HD], BF16, name="h_raw%d" % n) for n in range(HEADS)]
         wd_raw = [keep.tile([P, PACK, D], BF16, name="wd_raw%d" % n) for n in range(HEADS)]
-        h_codes = keep.tile([P, BLOCKS, HEADS, HD], U32, name="h_codes", align_bytes=64)
-        h_scales = keep.tile([P, BLOCKS, HEADS, HD], U8, name="h_scales", align_bytes=64)
-        wd_codes = keep.tile([P, HEADS, D], U32, name="wd_codes", align_bytes=64)
-        wd_scales = keep.tile([P, HEADS, D], U8, name="wd_scales", align_bytes=64)
+        h_codes = keep.tile([P, HEADS, BLOCKS * HD], U32, name="h_codes", align_bytes=64)
+        h_scales = keep.tile([P, HEADS, BLOCKS * HD], U8, name="h_scales", align_bytes=64)
+        wd_codes = keep.tile([P, CHUNKS, HEADS * CHUNK], U32, name="wd_codes", align_bytes=64)
+        wd_scales = keep.tile([P, CHUNKS, HEADS * CHUNK], U8, name="wd_scales", align_bytes=64)
         g_codes = keep.tile([P, HEADS, BLOCKS, K_PASS], U32, name="g_codes", align_bytes=64)
         g_scales = keep.tile([P, HEADS, BLOCKS, K_PASS], U8, name="g_scales", align_bytes=64)
 
         a_raw = {}
+        a_grouped = {}
         a_codes = {}
         a_scales = {}
+        h_grouped = {}
         h_scaled = {}
+        wd_grouped = {}
 
-        def load_unit(c, n):
-            if c == 0:
-                for cc in range(BLOCKS):
-                    for u in range(2):
-                        nc.sync.dma_start(
-                            out=h_raw[n][:, cc, 2 * u : 2 * u + 2, :],
-                            in_=h_view[cc, u, :, :, HD * n : HD * (n + 1)],
-                        )
-            a_raw[(c, n)] = raw.tile([P, PACK, S], BF16, name="a_raw")
+        def load_h(n):
+            for c in range(BLOCKS):
+                for u in range(2):
+                    nc.sync.dma_start(
+                        out=h_raw[n][:, c, 2 * u : 2 * u + 2, :],
+                        in_=h_view[c, u, :, :, HD * n : HD * (n + 1)],
+                    )
+
+        def load_adjacency(k):
+            c, n = units[k]
+            a_raw[k] = work.tile([P, PACK, S], BF16, name="a_raw", bufs=A_BUFS)
             nc.sync.dma_start(
-                out=a_raw[(c, n)][:].rearrange("p (u e) j -> p u (e j)", u=2),
-                in_=a_view[n, c, :, :, :],
+                out=a_raw[k][:].rearrange("p (u e) j -> p u (e j)", u=2), in_=a_view[n, c, :, :, :]
             )
-            if c == 1:
-                nc.sync.dma_start(
-                    out=wd_raw[n][:].rearrange("p (u e) d -> p u (e d)", u=2),
-                    in_=wd_view[n, :, :, :],
-                )
 
-        def quantise_h(n):
-            for cc in range(BLOCKS):
-                h_grouped = work.tile([P, HD, PACK], BF16, tag="grouped", bufs=3, align_bytes=64)
-                dst = h_grouped[:].rearrange("p (u e q) t -> p e u q t", u=2, e=2)
-                src = h_raw[n][:, cc, :, :].rearrange("p t (u q e) -> p e u q t", u=2, e=2)
+        def load_wd(n):
+            nc.sync.dma_start(
+                out=wd_raw[n][:].rearrange("p (u e) d -> p u (e d)", u=2), in_=wd_view[n, :, :, :]
+            )
+
+        def regroup_h(n):
+            h_grouped[n] = work.tile([P, BLOCKS, HD, PACK], BF16, name="h_grouped", tag="grouped", align_bytes=64)
+            for c in range(BLOCKS):
+                dst = h_grouped[n][:, c, :, :].rearrange("p (u e q) t -> p e u q t", u=2, e=2)
+                src = h_raw[n][:, c, :, :].rearrange("p t (u q e) -> p e u q t", u=2, e=2)
                 nc.vector.tensor_copy(out=dst[:, 0, :, :, :], in_=src[:, 0, :, :, :])
                 nc.scalar.copy(out=dst[:, 1, :, :, :], in_=src[:, 1, :, :, :])
-                nc.vector.quantize_mx(
-                    out=h_codes[:, cc, n, :].bitcast(FP8X4),
-                    scales=h_scales[:, cc, n, :],
-                    in_=h_grouped[:].rearrange("p x t -> p (x t)"),
-                )
 
-        def quantise_wd(n):
-            for dh in range(D // N_HALF):
-                cols = slice(N_HALF * dh, N_HALF * (dh + 1))
-                wd_grouped = work.tile([P, N_HALF, PACK], BF16, tag="grouped", bufs=3, align_bytes=64)
-                nc.vector.tensor_copy(
-                    out=wd_grouped[:].rearrange("p (x i) t -> p x t i", i=4),
-                    in_=wd_raw[n][:, :, cols].rearrange("p t (x i) -> p x t i", i=4),
-                )
-                nc.vector.quantize_mx(
-                    out=wd_codes[:, n, cols].bitcast(FP8X4),
-                    scales=wd_scales[:, n, cols],
-                    in_=wd_grouped[:].rearrange("p x t -> p (x t)"),
-                )
+        def quantise_h(n):
+            nc.vector.quantize_mx(
+                out=h_codes[:, n, :].bitcast(FP8X4),
+                scales=h_scales[:, n, :],
+                in_=h_grouped[n][:].rearrange("p c x t -> p (c x t)"),
+            )
 
-        def front(c, n):
-            a_codes[(c, n)] = work.tile([P, PACK, 2 * P], U32, name="a_codes", align_bytes=64)
-            a_scales[(c, n)] = work.tile([P, PACK, 2 * P], U8, name="a_scales", align_bytes=64)
+        def regroup_wd(q, n):
+            if n == 0:
+                wd_grouped[q] = work.tile([P, HEADS, CHUNK, PACK], BF16, name="wd_grouped", tag="grouped", align_bytes=64)
+            nc.vector.tensor_copy(
+                out=wd_grouped[q][:, n, :, :].rearrange("p (x i) t -> p x t i", i=4),
+                in_=wd_raw[n][:, :, CHUNK * q : CHUNK * (q + 1)].rearrange("p t (x i) -> p x t i", i=4),
+            )
+
+        def quantise_wd(q):
+            nc.vector.quantize_mx(
+                out=wd_codes[:, q, :].bitcast(FP8X4),
+                scales=wd_scales[:, q, :],
+                in_=wd_grouped[q][:].rearrange("p n x t -> p (n x t)"),
+            )
+
+        def transpose_adjacency(k):
             for ti in range(PACK):
-                a_words = a_raw[(c, n)][:, ti, :].bitcast(F32)
+                a_words = a_raw[k][:, ti, :].bitcast(F32)
                 at_ps = psum_tr.tile([P, BLOCKS, 2, P], F32, tag="tr")
-                for cp in range(BLOCKS):
-                    for up in range(2):
-                        w0 = 256 * cp + P * up
-                        nc.tensor.transpose(at_ps[:, cp, up, :], a_words[:, w0 : w0 + P], ident[:])
-                a_grouped = work.tile([P, BLOCKS, P, PACK], BF16, bufs=4, align_bytes=64)
+                for c in range(BLOCKS):
+                    for u in range(2):
+                        w0 = (2 * c + u) * P
+                        nc.tensor.transpose(at_ps[:, c, u, :], a_words[:, w0 : w0 + P], ident[:])
+                a_grouped[(k, ti)] = work.tile([P, BLOCKS, P, PACK], BF16, name="a_grouped", bufs=PACK, align_bytes=64)
                 nc.scalar.copy(
-                    out=a_grouped[:].bitcast(F32),
-                    in_=at_ps[:].rearrange("p c u i -> p c i u"),
+                    out=a_grouped[(k, ti)][:].bitcast(F32), in_=at_ps[:].rearrange("p c u i -> p c i u")
                 )
+
+        def quantise_adjacency(k):
+            a_codes[k] = work.tile([P, PACK, BLOCKS * P], U32, name="a_codes", align_bytes=64)
+            a_scales[k] = work.tile([P, PACK, BLOCKS * P], U8, name="a_scales", align_bytes=64)
+            for ti in range(PACK):
                 nc.vector.quantize_mx(
-                    out=a_codes[(c, n)][:, ti, :].bitcast(FP8X4),
-                    scales=a_scales[(c, n)][:, ti, :],
-                    in_=a_grouped[:].rearrange("p c i t -> p (c i t)"),
+                    out=a_codes[k][:, ti, :].bitcast(FP8X4),
+                    scales=a_scales[k][:, ti, :],
+                    in_=a_grouped[(k, ti)][:].rearrange("p c i t -> p (c i t)"),
                 )
-            h_scaled[(c, n)] = work.tile([P, PACK * P, PACK], F32, name="h_scaled")
+
+        def transpose_h(k):
+            c, n = units[k]
+            h_scaled[k] = work.tile([P, PACK * P, PACK], F32, name="h_scaled")
             for pair in range(2):
                 ht_ps = psum_tr.tile([P, 2, 2 * P], F32, tag="tr")
                 for ti2 in range(2):
                     h_words = h_raw[n][:, c, 2 * pair + ti2, :].bitcast(F32)
-                    for uf in range(2):
+                    for u in range(2):
                         nc.tensor.transpose(
-                            ht_ps[:, uf, P * ti2 : P * (ti2 + 1)],
-                            h_words[:, P * uf : P * (uf + 1)],
-                            ident[:],
+                            ht_ps[:, u, P * ti2 : P * (ti2 + 1)], h_words[:, P * u : P * (u + 1)], ident[:]
                         )
                 nc.scalar.activation(
-                    out=h_scaled[(c, n)][:, 2 * P * pair : 2 * P * (pair + 1), :].rearrange(
-                        "p x (u e) -> p x u e", e=2
-                    ),
+                    out=h_scaled[k][:, 2 * P * pair : 2 * P * (pair + 1), :].rearrange("p x (u e) -> p x u e", e=2),
                     in_=ht_ps[:].bitcast(BF16).rearrange("p u (x e) -> p x u e", e=2),
                     func=ACT.Copy,
                     scale=one_plus_eps[:, n : n + 1],
                 )
 
-        def back(c, n):
+        def mix(k):
+            c, n = units[k]
             g_grouped = work.tile([P, PACK * P, PACK], BF16, align_bytes=64)
             for ti in range(PACK):
                 agg_ps = psum_acc.tile([P, PACK, P], F32, tag="acc")
                 for tf in range(PACK):
                     for cp in range(BLOCKS):
+                        f_cols = slice(HD * cp + P * tf, HD * cp + P * (tf + 1))
+                        i_cols = slice(P * cp, P * (cp + 1))
                         nc.tensor.matmul_mx(
                             out=agg_ps[:, tf, :],
-                            lhsT=h_codes[:, cp, n, P * tf : P * (tf + 1)].bitcast(FP8X4),
-                            lhsT_scale=h_scales[:, cp, n, P * tf : P * (tf + 1)],
-                            rhs=a_codes[(c, n)][:, ti, P * cp : P * (cp + 1)].bitcast(FP8X4),
-                            rhs_scale=a_scales[(c, n)][:, ti, P * cp : P * (cp + 1)],
+                            lhsT=h_codes[:, n, f_cols].bitcast(FP8X4),
+                            lhsT_scale=h_scales[:, n, f_cols],
+                            rhs=a_codes[k][:, ti, i_cols].bitcast(FP8X4),
+                            rhs_scale=a_scales[k][:, ti, i_cols],
                             start=(cp == 0),
                             stop=(cp == BLOCKS - 1),
                         )
@@ -169,7 +184,7 @@ def tile_llamamlp_halfwaygin_pa_kernel(tc, h_inter, adjacency, Wd, eps, alpha, o
                     out=g_grouped[:, P * ti : P * (ti + 1), :],
                     in0=agg_ps[:].rearrange("p t i -> p i t"),
                     scalar=alpha_f[:, n : n + 1],
-                    in1=h_scaled[(c, n)][:, P * ti : P * (ti + 1), :],
+                    in1=h_scaled[k][:, P * ti : P * (ti + 1), :],
                     op0=ALU.mult,
                     op1=ALU.add,
                 )
@@ -179,44 +194,59 @@ def tile_llamamlp_halfwaygin_pa_kernel(tc, h_inter, adjacency, Wd, eps, alpha, o
                 in_=g_grouped[:].rearrange("p x t -> p (x t)"),
             )
 
-        def down_projection(c):
-            for ti in range(PACK):
-                out_sb = work.tile([P, D], F32, bufs=3)
-                for dh in range(D // N_HALF):
-                    cols = slice(N_HALF * dh, N_HALF * (dh + 1))
-                    out_ps = psum_acc.tile([P, N_HALF], F32, tag="acc")
-                    for n in range(HEADS):
-                        nc.tensor.matmul_mx(
-                            out=out_ps[:],
-                            lhsT=g_codes[:, n, c, P * ti : P * (ti + 1)].bitcast(FP8X4),
-                            lhsT_scale=g_scales[:, n, c, P * ti : P * (ti + 1)],
-                            rhs=wd_codes[:, n, cols].bitcast(FP8X4),
-                            rhs_scale=wd_scales[:, n, cols],
-                            start=(n == 0),
-                            stop=(n == HEADS - 1),
-                        )
-                    if dh == 0:
-                        nc.scalar.copy(out=out_sb[:, cols], in_=out_ps[:])
-                    else:
-                        nc.vector.tensor_copy(out=out_sb[:, cols], in_=out_ps[:])
-                nc.sync.dma_start(out=out_view[c, ti // 2, :, ti % 2, :], in_=out_sb[:])
+        def project(q):
+            for c in range(BLOCKS):
+                for u in range(2):
+                    out_ps = psum_acc.tile([P, 2, CHUNK], F32, tag="acc")
+                    for e in range(2):
+                        i_cols = slice(P * (2 * u + e), P * (2 * u + e + 1))
+                        for n in range(HEADS):
+                            d_cols = slice(CHUNK * n, CHUNK * (n + 1))
+                            nc.tensor.matmul_mx(
+                                out=out_ps[:, e, :],
+                                lhsT=g_codes[:, n, c, i_cols].bitcast(FP8X4),
+                                lhsT_scale=g_scales[:, n, c, i_cols],
+                                rhs=wd_codes[:, q, d_cols].bitcast(FP8X4),
+                                rhs_scale=wd_scales[:, q, d_cols],
+                                start=(n == 0),
+                                stop=(n == HEADS - 1),
+                            )
+                    out_sb = work.tile([P, 2, CHUNK], F32, bufs=4)
+                    nc.scalar.copy(out=out_sb[:], in_=out_ps[:])
+                    nc.sync.dma_start(out=out_view[c, u, :, :, CHUNK * q : CHUNK * (q + 1)], in_=out_sb[:])
 
-        units = [(c, n) for c in range(BLOCKS) for n in range(HEADS)]
-        ahead = 4
-        for k in range(ahead):
-            load_unit(*units[k])
+        for n in range(HEADS):
+            load_h(n)
+            load_adjacency(n)
+
+        regroup_h(0)
         quantise_h(0)
-        front(*units[0])
-        for k in range(len(units)):
-            c, n = units[k]
-            if k + ahead < len(units):
-                load_unit(*units[k + ahead])
-            if k + 1 < len(units):
-                if units[k + 1][0] == 0:
-                    quantise_h(units[k + 1][1])
-                front(*units[k + 1])
-            back(c, n)
-            if c == 1:
-                quantise_wd(n)
-        for c in range(BLOCKS):
-            down_projection(c)
+        last = len(units) - 1
+        for k in range(-1, last + 1):
+            if k < last:
+                transpose_adjacency(k + 1)
+                if k + 1 + A_BUFS <= last:
+                    load_adjacency(k + 1 + A_BUFS)
+                    if k + 1 + A_BUFS == last:
+                        for n in range(HEADS):
+                            load_wd(n)
+            if k + 2 < HEADS:
+                regroup_h(k + 2)
+            if k >= HEADS:
+                regroup_wd(0, k - HEADS)
+            if k == last:
+                quantise_wd(0)
+            if k < last:
+                quantise_adjacency(k + 1)
+                transpose_h(k + 1)
+            if k >= 0:
+                mix(k)
+            if k + 2 < HEADS:
+                quantise_h(k + 2)
+
+        for q in range(CHUNKS):
+            if q + 1 < CHUNKS:
+                for n in range(HEADS):
+                    regroup_wd(q + 1, n)
+                quantise_wd(q + 1)
+            project(q)

@@ -22,6 +22,9 @@ BLOCKS = S // K_PASS
 CHUNK = 256
 CHUNKS = D // CHUNK
 A_BUFS = 4
+GROUPED_BUFS = 3
+HALVES = 1
+RUN = PACK // HALVES
 
 FLOPS = 2 * HEADS * S * S * HD + 2 * S * HEADS * HD * D
 
@@ -34,7 +37,7 @@ def tile_llamamlp_halfwaygin_pa_kernel(tc, h_inter, adjacency, Wd, eps, alpha, o
     wd_view = Wd.rearrange("(n u p e) d -> n p u (e d)", n=HEADS, u=2, p=P, e=2)
     out_view = out.rearrange("b (c u p e) d -> (b c) u p e d", c=BLOCKS, u=2, p=P, e=2)
 
-    units = [(c, n) for c in range(BLOCKS) for n in range(HEADS)]
+    units = [(c, n) for n in range(HEADS) for c in range(BLOCKS)]
 
     with ExitStack() as ctx:
         keep = ctx.enter_context(tc.tile_pool(name="keep", bufs=1))
@@ -69,6 +72,7 @@ def tile_llamamlp_halfwaygin_pa_kernel(tc, h_inter, adjacency, Wd, eps, alpha, o
         a_scales = {}
         h_grouped = {}
         h_scaled = {}
+        g_grouped = {}
         wd_grouped = {}
 
         def load_h(n):
@@ -91,13 +95,15 @@ def tile_llamamlp_halfwaygin_pa_kernel(tc, h_inter, adjacency, Wd, eps, alpha, o
                 out=wd_raw[n][:].rearrange("p (u e) d -> p u (e d)", u=2), in_=wd_view[n, :, :, :]
             )
 
-        def regroup_h(n):
-            h_grouped[n] = work.tile([P, BLOCKS, HD, PACK], BF16, name="h_grouped", tag="grouped", align_bytes=64)
-            for c in range(BLOCKS):
-                dst = h_grouped[n][:, c, :, :].rearrange("p (u e q) t -> p e u q t", u=2, e=2)
-                src = h_raw[n][:, c, :, :].rearrange("p t (u q e) -> p e u q t", u=2, e=2)
-                nc.vector.tensor_copy(out=dst[:, 0, :, :, :], in_=src[:, 0, :, :, :])
-                nc.scalar.copy(out=dst[:, 1, :, :, :], in_=src[:, 1, :, :, :])
+        def regroup_h(n, c):
+            if c == 0:
+                h_grouped[n] = work.tile(
+                    [P, BLOCKS, HD, PACK], BF16, name="h_grouped", tag="grouped", bufs=GROUPED_BUFS, align_bytes=64
+                )
+            dst = h_grouped[n][:, c, :, :].rearrange("p (u e q) t -> p e u q t", u=2, e=2)
+            src = h_raw[n][:, c, :, :].rearrange("p t (u q e) -> p e u q t", u=2, e=2)
+            nc.vector.tensor_copy(out=dst[:, 0, :, :, :], in_=src[:, 0, :, :, :])
+            nc.scalar.copy(out=dst[:, 1, :, :, :], in_=src[:, 1, :, :, :])
 
         def quantise_h(n):
             nc.vector.quantize_mx(
@@ -106,10 +112,12 @@ def tile_llamamlp_halfwaygin_pa_kernel(tc, h_inter, adjacency, Wd, eps, alpha, o
                 in_=h_grouped[n][:].rearrange("p c x t -> p (c x t)"),
             )
 
-        def regroup_wd(q, n):
+        def regroup_wd(q, n, copy):
             if n == 0:
-                wd_grouped[q] = work.tile([P, HEADS, CHUNK, PACK], BF16, name="wd_grouped", tag="grouped", align_bytes=64)
-            nc.vector.tensor_copy(
+                wd_grouped[q] = work.tile(
+                    [P, HEADS, CHUNK, PACK], BF16, name="wd_grouped", tag="grouped", bufs=GROUPED_BUFS, align_bytes=64
+                )
+            copy(
                 out=wd_grouped[q][:, n, :, :].rearrange("p (x i) t -> p x t i", i=4),
                 in_=wd_raw[n][:, :, CHUNK * q : CHUNK * (q + 1)].rearrange("p t (x i) -> p x t i", i=4),
             )
@@ -121,8 +129,8 @@ def tile_llamamlp_halfwaygin_pa_kernel(tc, h_inter, adjacency, Wd, eps, alpha, o
                 in_=wd_grouped[q][:].rearrange("p n x t -> p (n x t)"),
             )
 
-        def transpose_adjacency(k):
-            for ti in range(PACK):
+        def transpose_adjacency(k, half):
+            for ti in range(RUN * half, RUN * (half + 1)):
                 a_words = a_raw[k][:, ti, :].bitcast(F32)
                 at_ps = psum_tr.tile([P, BLOCKS, 2, P], F32, tag="tr")
                 for c in range(BLOCKS):
@@ -134,27 +142,27 @@ def tile_llamamlp_halfwaygin_pa_kernel(tc, h_inter, adjacency, Wd, eps, alpha, o
                     out=a_grouped[(k, ti)][:].bitcast(F32), in_=at_ps[:].rearrange("p c u i -> p c i u")
                 )
 
-        def quantise_adjacency(k):
-            a_codes[k] = work.tile([P, PACK, BLOCKS * P], U32, name="a_codes", align_bytes=64)
-            a_scales[k] = work.tile([P, PACK, BLOCKS * P], U8, name="a_scales", align_bytes=64)
-            for ti in range(PACK):
+        def quantise_adjacency(k, half):
+            if half == 0:
+                a_codes[k] = work.tile([P, PACK, BLOCKS * P], U32, name="a_codes", align_bytes=64)
+                a_scales[k] = work.tile([P, PACK, BLOCKS * P], U8, name="a_scales", align_bytes=64)
+            for ti in range(RUN * half, RUN * (half + 1)):
                 nc.vector.quantize_mx(
                     out=a_codes[k][:, ti, :].bitcast(FP8X4),
                     scales=a_scales[k][:, ti, :],
                     in_=a_grouped[(k, ti)][:].rearrange("p c i t -> p (c i t)"),
                 )
 
-        def transpose_h(k):
+        def transpose_h(k, half):
             c, n = units[k]
-            h_scaled[k] = work.tile([P, PACK * P, PACK], F32, name="h_scaled")
-            for pair in range(2):
+            if half == 0:
+                h_scaled[k] = work.tile([P, PACK * P, PACK], F32, name="h_scaled")
+            for pair in range(RUN * half // 2, RUN * (half + 1) // 2):
                 ht_ps = psum_tr.tile([P, 2, 2 * P], F32, tag="tr")
-                for ti2 in range(2):
-                    h_words = h_raw[n][:, c, 2 * pair + ti2, :].bitcast(F32)
+                for r in range(2):
+                    h_words = h_raw[n][:, c, 2 * pair + r, :].bitcast(F32)
                     for u in range(2):
-                        nc.tensor.transpose(
-                            ht_ps[:, u, P * ti2 : P * (ti2 + 1)], h_words[:, P * u : P * (u + 1)], ident[:]
-                        )
+                        nc.tensor.transpose(ht_ps[:, u, P * r : P * (r + 1)], h_words[:, P * u : P * (u + 1)], ident[:])
                 nc.scalar.activation(
                     out=h_scaled[k][:, 2 * P * pair : 2 * P * (pair + 1), :].rearrange("p x (u e) -> p x u e", e=2),
                     in_=ht_ps[:].bitcast(BF16).rearrange("p u (x e) -> p x u e", e=2),
@@ -162,10 +170,11 @@ def tile_llamamlp_halfwaygin_pa_kernel(tc, h_inter, adjacency, Wd, eps, alpha, o
                     scale=one_plus_eps[:, n : n + 1],
                 )
 
-        def mix(k):
+        def mix(k, half):
             c, n = units[k]
-            g_grouped = work.tile([P, PACK * P, PACK], BF16, align_bytes=64)
-            for ti in range(PACK):
+            if half == 0:
+                g_grouped[k] = work.tile([P, PACK * P, PACK], BF16, name="g_grouped", align_bytes=64)
+            for ti in range(RUN * half, RUN * (half + 1)):
                 agg_ps = psum_acc.tile([P, PACK, P], F32, tag="acc")
                 for tf in range(PACK):
                     for cp in range(BLOCKS):
@@ -181,17 +190,20 @@ def tile_llamamlp_halfwaygin_pa_kernel(tc, h_inter, adjacency, Wd, eps, alpha, o
                             stop=(cp == BLOCKS - 1),
                         )
                 nc.vector.scalar_tensor_tensor(
-                    out=g_grouped[:, P * ti : P * (ti + 1), :],
+                    out=g_grouped[k][:, P * ti : P * (ti + 1), :],
                     in0=agg_ps[:].rearrange("p t i -> p i t"),
                     scalar=alpha_f[:, n : n + 1],
                     in1=h_scaled[k][:, P * ti : P * (ti + 1), :],
                     op0=ALU.mult,
                     op1=ALU.add,
                 )
+
+        def quantise_g(k):
+            c, n = units[k]
             nc.vector.quantize_mx(
                 out=g_codes[:, n, c, :].bitcast(FP8X4),
                 scales=g_scales[:, n, c, :],
-                in_=g_grouped[:].rearrange("p x t -> p (x t)"),
+                in_=g_grouped[k][:].rearrange("p x t -> p (x t)"),
             )
 
         def project(q):
@@ -217,36 +229,44 @@ def tile_llamamlp_halfwaygin_pa_kernel(tc, h_inter, adjacency, Wd, eps, alpha, o
 
         for n in range(HEADS):
             load_h(n)
-            load_adjacency(n)
+            for k in range(BLOCKS * n, min(BLOCKS * (n + 1), A_BUFS)):
+                load_adjacency(k)
 
-        regroup_h(0)
+        for c in range(BLOCKS):
+            regroup_h(0, c)
         quantise_h(0)
         last = len(units) - 1
         for k in range(-1, last + 1):
-            if k < last:
-                transpose_adjacency(k + 1)
-                if k + 1 + A_BUFS <= last:
-                    load_adjacency(k + 1 + A_BUFS)
-                    if k + 1 + A_BUFS == last:
-                        for n in range(HEADS):
-                            load_wd(n)
-            if k + 2 < HEADS:
-                regroup_h(k + 2)
-            if k >= HEADS:
-                regroup_wd(0, k - HEADS)
+            next_head = k // BLOCKS + 1
+            if last - HEADS <= k < last:
+                regroup_wd(0, k - (last - HEADS), nc.vector.tensor_copy)
             if k == last:
+                for n in range(HEADS):
+                    regroup_wd(1, n, nc.scalar.copy)
+            for half in range(HALVES):
+                if k < last:
+                    transpose_adjacency(k + 1, half)
+                if half == HALVES - 1 and k >= 0 and next_head < HEADS:
+                    regroup_h(next_head, k % BLOCKS)
+                if k < last:
+                    quantise_adjacency(k + 1, half)
+                    transpose_h(k + 1, half)
+                if k >= 0:
+                    mix(k, half)
+            if k + 1 + A_BUFS <= last:
+                load_adjacency(k + 1 + A_BUFS)
+                load_wd(k + 1)
+            if k == last - 1:
                 quantise_wd(0)
-            if k < last:
-                quantise_adjacency(k + 1)
-                transpose_h(k + 1)
             if k >= 0:
-                mix(k)
-            if k + 2 < HEADS:
-                quantise_h(k + 2)
+                quantise_g(k)
+            if k >= 0 and next_head < HEADS and k % BLOCKS == BLOCKS - 1:
+                quantise_h(next_head)
+        quantise_wd(1)
 
         for q in range(CHUNKS):
-            if q + 1 < CHUNKS:
+            if 2 <= q + 1 < CHUNKS:
                 for n in range(HEADS):
-                    regroup_wd(q + 1, n)
+                    regroup_wd(q + 1, n, nc.vector.tensor_copy)
                 quantise_wd(q + 1)
             project(q)

@@ -23,8 +23,6 @@ CHUNK = 256
 CHUNKS = D // CHUNK
 A_BUFS = 4
 GROUPED_BUFS = 3
-HALVES = 1
-RUN = PACK // HALVES
 
 FLOPS = 2 * HEADS * S * S * HD + 2 * S * HEADS * HD * D
 
@@ -54,8 +52,10 @@ def tile_llamamlp_halfwaygin_pa_kernel(tc, h_inter, adjacency, Wd, eps, alpha, o
         nc.scalar.dma_start(out=alpha_bf[:], in_=alpha.partition_broadcast(P))
         one_plus_eps = keep.tile([P, HEADS], F32, name="one_plus_eps")
         alpha_f = keep.tile([P, HEADS], F32, name="alpha_f")
-        nc.vector.tensor_scalar_add(out=one_plus_eps[:], in0=eps_bf[:], scalar1=1.0)
-        nc.vector.tensor_copy(out=alpha_f[:], in_=alpha_bf[:])
+        warm = keep.tile([P, 8], F32, name="warm")
+        nc.vector.memset(warm[:], 0.0)
+        warm_out = keep.tile([P, 8], F32, name="warm_out")
+        nc.scalar.copy(out=warm_out[:], in_=warm[:])
 
         h_raw = [keep.tile([P, BLOCKS, PACK, HD], BF16, name="h_raw%d" % n) for n in range(HEADS)]
         wd_raw = [keep.tile([P, PACK, D], BF16, name="wd_raw%d" % n) for n in range(HEADS)]
@@ -83,33 +83,36 @@ def tile_llamamlp_halfwaygin_pa_kernel(tc, h_inter, adjacency, Wd, eps, alpha, o
                         in_=h_view[c, u, :, :, HD * n : HD * (n + 1)],
                     )
 
-        def load_adjacency(k):
+        def load_adjacency(k, halves=(0, 1)):
             c, n = units[k]
-            a_raw[k] = work.tile([P, PACK, S], BF16, name="a_raw", bufs=A_BUFS)
-            nc.sync.dma_start(
-                out=a_raw[k][:].rearrange("p (u e) j -> p u (e j)", u=2), in_=a_view[n, c, :, :, :]
-            )
+            if halves[0] == 0:
+                a_raw[k] = work.tile([P, PACK, S], BF16, name="a_raw", bufs=A_BUFS)
+            for u in halves:
+                nc.sync.dma_start(
+                    out=a_raw[k][:, 2 * u : 2 * u + 2, :].rearrange("p e j -> p (e j)"), in_=a_view[n, c, :, u, :]
+                )
 
         def load_wd(n):
             nc.sync.dma_start(
                 out=wd_raw[n][:].rearrange("p (u e) d -> p u (e d)", u=2), in_=wd_view[n, :, :, :]
             )
 
-        def regroup_h(n, c):
+        def regroup_h(n, c, copy_even, copy_odd):
             if c == 0:
                 h_grouped[n] = work.tile(
                     [P, BLOCKS, HD, PACK], BF16, name="h_grouped", tag="grouped", bufs=GROUPED_BUFS, align_bytes=64
                 )
             dst = h_grouped[n][:, c, :, :].rearrange("p (u e q) t -> p e u q t", u=2, e=2)
             src = h_raw[n][:, c, :, :].rearrange("p t (u q e) -> p e u q t", u=2, e=2)
-            nc.vector.tensor_copy(out=dst[:, 0, :, :, :], in_=src[:, 0, :, :, :])
-            nc.scalar.copy(out=dst[:, 1, :, :, :], in_=src[:, 1, :, :, :])
+            copy_even(out=dst[:, 0, :, :, :], in_=src[:, 0, :, :, :])
+            copy_odd(out=dst[:, 1, :, :, :], in_=src[:, 1, :, :, :])
 
-        def quantise_h(n):
+        def quantise_h(n, c):
+            cols = slice(HD * c, HD * (c + 1))
             nc.vector.quantize_mx(
-                out=h_codes[:, n, :].bitcast(FP8X4),
-                scales=h_scales[:, n, :],
-                in_=h_grouped[n][:].rearrange("p c x t -> p (c x t)"),
+                out=h_codes[:, n, cols].bitcast(FP8X4),
+                scales=h_scales[:, n, cols],
+                in_=h_grouped[n][:, c, :, :].rearrange("p x t -> p (x t)"),
             )
 
         def regroup_wd(q, n, copy):
@@ -129,8 +132,8 @@ def tile_llamamlp_halfwaygin_pa_kernel(tc, h_inter, adjacency, Wd, eps, alpha, o
                 in_=wd_grouped[q][:].rearrange("p n x t -> p (n x t)"),
             )
 
-        def transpose_adjacency(k, half):
-            for ti in range(RUN * half, RUN * (half + 1)):
+        def transpose_adjacency(k, tiles):
+            for ti in tiles:
                 a_words = a_raw[k][:, ti, :].bitcast(F32)
                 at_ps = psum_tr.tile([P, BLOCKS, 2, P], F32, tag="tr")
                 for c in range(BLOCKS):
@@ -142,22 +145,21 @@ def tile_llamamlp_halfwaygin_pa_kernel(tc, h_inter, adjacency, Wd, eps, alpha, o
                     out=a_grouped[(k, ti)][:].bitcast(F32), in_=at_ps[:].rearrange("p c u i -> p c i u")
                 )
 
-        def quantise_adjacency(k, half):
-            if half == 0:
+        def quantise_adjacency(k, tiles):
+            if tiles[0] == 0:
                 a_codes[k] = work.tile([P, PACK, BLOCKS * P], U32, name="a_codes", align_bytes=64)
                 a_scales[k] = work.tile([P, PACK, BLOCKS * P], U8, name="a_scales", align_bytes=64)
-            for ti in range(RUN * half, RUN * (half + 1)):
+            for ti in tiles:
                 nc.vector.quantize_mx(
                     out=a_codes[k][:, ti, :].bitcast(FP8X4),
                     scales=a_scales[k][:, ti, :],
                     in_=a_grouped[(k, ti)][:].rearrange("p c i t -> p (c i t)"),
                 )
 
-        def transpose_h(k, half):
+        def transpose_h(k):
             c, n = units[k]
-            if half == 0:
-                h_scaled[k] = work.tile([P, PACK * P, PACK], F32, name="h_scaled")
-            for pair in range(RUN * half // 2, RUN * (half + 1) // 2):
+            h_scaled[k] = work.tile([P, PACK * P, PACK], F32, name="h_scaled")
+            for pair in range(PACK // 2):
                 ht_ps = psum_tr.tile([P, 2, 2 * P], F32, tag="tr")
                 for r in range(2):
                     h_words = h_raw[n][:, c, 2 * pair + r, :].bitcast(F32)
@@ -170,11 +172,10 @@ def tile_llamamlp_halfwaygin_pa_kernel(tc, h_inter, adjacency, Wd, eps, alpha, o
                     scale=one_plus_eps[:, n : n + 1],
                 )
 
-        def mix(k, half):
+        def mix(k):
             c, n = units[k]
-            if half == 0:
-                g_grouped[k] = work.tile([P, PACK * P, PACK], BF16, name="g_grouped", align_bytes=64)
-            for ti in range(RUN * half, RUN * (half + 1)):
+            g_grouped[k] = work.tile([P, PACK * P, PACK], BF16, name="g_grouped", align_bytes=64)
+            for ti in range(PACK):
                 agg_ps = psum_acc.tile([P, PACK, P], F32, tag="acc")
                 for tf in range(PACK):
                     for cp in range(BLOCKS):
@@ -206,10 +207,13 @@ def tile_llamamlp_halfwaygin_pa_kernel(tc, h_inter, adjacency, Wd, eps, alpha, o
                 in_=g_grouped[k][:].rearrange("p x t -> p (x t)"),
             )
 
-        def project(q):
+        def project(q, copies):
             for c in range(BLOCKS):
                 for u in range(2):
-                    out_ps = psum_acc.tile([P, 2, CHUNK], F32, tag="acc")
+                    if u == 0:
+                        out_ps = psum_tr.tile([P, 2, CHUNK], F32, tag="tr")
+                    else:
+                        out_ps = psum_acc.tile([P, 2, CHUNK], F32, tag="acc")
                     for e in range(2):
                         i_cols = slice(P * (2 * u + e), P * (2 * u + e + 1))
                         for n in range(HEADS):
@@ -224,49 +228,69 @@ def tile_llamamlp_halfwaygin_pa_kernel(tc, h_inter, adjacency, Wd, eps, alpha, o
                                 stop=(n == HEADS - 1),
                             )
                     out_sb = work.tile([P, 2, CHUNK], F32, bufs=4)
-                    nc.scalar.copy(out=out_sb[:], in_=out_ps[:])
+                    copies[u](out=out_sb[:], in_=out_ps[:])
                     nc.sync.dma_start(out=out_view[c, u, :, :, CHUNK * q : CHUNK * (q + 1)], in_=out_sb[:])
 
-        for n in range(HEADS):
-            load_h(n)
-            for k in range(BLOCKS * n, min(BLOCKS * (n + 1), A_BUFS)):
-                load_adjacency(k)
-
-        for c in range(BLOCKS):
-            regroup_h(0, c)
-        quantise_h(0)
+        vcopy = nc.vector.tensor_copy
+        scopy = nc.scalar.copy
         last = len(units) - 1
-        for k in range(-1, last + 1):
+        all_tiles = range(PACK)
+
+        load_adjacency(0, (0,))
+        load_h(0)
+        load_adjacency(0, (1,))
+        load_adjacency(1)
+        load_h(1)
+        load_adjacency(2)
+        load_adjacency(3)
+        load_h(2)
+
+        transpose_adjacency(0, (0, 1))
+        regroup_h(0, 0, vcopy, scopy)
+        quantise_adjacency(0, (0,))
+        nc.vector.tensor_scalar_add(out=one_plus_eps[:], in0=eps_bf[:], scalar1=1.0)
+        nc.vector.tensor_copy(out=alpha_f[:], in_=alpha_bf[:])
+        regroup_h(0, 1, vcopy, scopy)
+        quantise_h(0, 0)
+        quantise_adjacency(0, (1,))
+        quantise_h(0, 1)
+        transpose_adjacency(0, (2, 3))
+        transpose_h(0)
+        quantise_adjacency(0, (2, 3))
+
+        for k in range(last + 1):
             next_head = k // BLOCKS + 1
+            if k < last:
+                transpose_adjacency(k + 1, all_tiles)
+                transpose_h(k + 1)
+            if k + 1 + A_BUFS <= last + 1:
+                if k == 1:
+                    load_h(3)
+                load_adjacency(k + A_BUFS)
+                load_wd(k)
             if last - HEADS <= k < last:
-                regroup_wd(0, k - (last - HEADS), nc.vector.tensor_copy)
+                regroup_wd(0, k - (last - HEADS), vcopy)
+            if next_head < HEADS:
+                regroup_h(next_head, k % BLOCKS, vcopy, scopy)
             if k == last:
                 for n in range(HEADS):
-                    regroup_wd(1, n, nc.scalar.copy)
-            for half in range(HALVES):
-                if k < last:
-                    transpose_adjacency(k + 1, half)
-                if half == HALVES - 1 and k >= 0 and next_head < HEADS:
-                    regroup_h(next_head, k % BLOCKS)
-                if k < last:
-                    quantise_adjacency(k + 1, half)
-                    transpose_h(k + 1, half)
-                if k >= 0:
-                    mix(k, half)
-            if k + 1 + A_BUFS <= last:
-                load_adjacency(k + 1 + A_BUFS)
-                load_wd(k + 1)
-            if k == last - 1:
+                    regroup_wd(1, n, scopy)
+            if k > 0:
+                if (k - 1) // BLOCKS + 1 < HEADS:
+                    quantise_h((k - 1) // BLOCKS + 1, (k - 1) % BLOCKS)
+                quantise_g(k - 1)
+            if k == last:
                 quantise_wd(0)
-            if k >= 0:
-                quantise_g(k)
-            if k >= 0 and next_head < HEADS and k % BLOCKS == BLOCKS - 1:
-                quantise_h(next_head)
+            if k < last:
+                quantise_adjacency(k + 1, all_tiles)
+            mix(k)
+        regroup_wd(2, 0, vcopy)
+        quantise_g(last)
         quantise_wd(1)
 
         for q in range(CHUNKS):
             if 2 <= q + 1 < CHUNKS:
-                for n in range(HEADS):
-                    regroup_wd(q + 1, n, nc.vector.tensor_copy)
+                for n in range(1 if q == 1 else 0, HEADS):
+                    regroup_wd(q + 1, n, vcopy)
                 quantise_wd(q + 1)
-            project(q)
+            project(q, (scopy, vcopy if q == CHUNKS - 1 else scopy))

@@ -40,12 +40,13 @@ def tile_llamamlp_halfwaygin_pa_kernel(tc, h_inter, adjacency, Wd, eps, alpha, o
     with ExitStack() as ctx:
         keep = ctx.enter_context(tc.tile_pool(name="keep", bufs=1))
         work = ctx.enter_context(tc.tile_pool(name="work", bufs=2))
-        psum_tr = ctx.enter_context(tc.psum_pool(name="psum_tr", bufs=4))
-        psum_acc = ctx.enter_context(tc.psum_pool(name="psum_acc", bufs=4))
+        psum = ctx.enter_context(tc.psum_pool(name="psum", bufs=8))
         ctx.enter_context(tc.manual_schedule())
 
         ident = keep.tile([P, P], F32, name="ident")
         make_identity(nc, ident[:])
+        ident_bf = keep.tile([P, P], BF16, name="ident_bf")
+        make_identity(nc, ident_bf[:])
         eps_bf = keep.tile([P, HEADS], BF16, name="eps_bf")
         alpha_bf = keep.tile([P, HEADS], BF16, name="alpha_bf")
         nc.scalar.dma_start(out=eps_bf[:], in_=eps.partition_broadcast(P))
@@ -97,15 +98,22 @@ def tile_llamamlp_halfwaygin_pa_kernel(tc, h_inter, adjacency, Wd, eps, alpha, o
                 out=wd_raw[n][:].rearrange("p (u e) d -> p u (e d)", u=2), in_=wd_view[n, :, :, :]
             )
 
-        def regroup_h(n, c, copy_even, copy_odd):
+        def regroup_h(n, c):
             if c == 0:
                 h_grouped[n] = work.tile(
                     [P, BLOCKS, HD, PACK], BF16, name="h_grouped", tag="grouped", bufs=GROUPED_BUFS, align_bytes=64
                 )
             dst = h_grouped[n][:, c, :, :].rearrange("p (u e q) t -> p e u q t", u=2, e=2)
             src = h_raw[n][:, c, :, :].rearrange("p t (u q e) -> p e u q t", u=2, e=2)
-            copy_even(out=dst[:, 0, :, :, :], in_=src[:, 0, :, :, :])
-            copy_odd(out=dst[:, 1, :, :, :], in_=src[:, 1, :, :, :])
+            nc.vector.tensor_copy(out=dst[:, 0, :, :, :], in_=src[:, 0, :, :, :])
+            odd_ps = psum.tile([P, 2, P, PACK], BF16, tag="bank")
+            for u in range(2):
+                nc.tensor.matmul(odd_ps[:, u, :, :], ident_bf[:], src[:, 1, u, :, :], start=True, stop=True)
+            words = h_grouped[n][:, c, :, :].rearrange("p x t -> p (x t)").bitcast(F32)
+            nc.scalar.copy(
+                out=words.rearrange("p (u e w) -> p e u w", u=2, e=2)[:, 1, :, :],
+                in_=odd_ps[:].rearrange("p u q t -> p (u q t)").bitcast(F32).rearrange("p (u w) -> p u w", u=2),
+            )
 
         def quantise_h(n, c):
             cols = slice(HD * c, HD * (c + 1))
@@ -135,7 +143,7 @@ def tile_llamamlp_halfwaygin_pa_kernel(tc, h_inter, adjacency, Wd, eps, alpha, o
         def transpose_adjacency(k, tiles):
             for ti in tiles:
                 a_words = a_raw[k][:, ti, :].bitcast(F32)
-                at_ps = psum_tr.tile([P, BLOCKS, 2, P], F32, tag="tr")
+                at_ps = psum.tile([P, BLOCKS, 2, P], F32, tag="bank")
                 for c in range(BLOCKS):
                     for u in range(2):
                         w0 = (2 * c + u) * P
@@ -160,7 +168,7 @@ def tile_llamamlp_halfwaygin_pa_kernel(tc, h_inter, adjacency, Wd, eps, alpha, o
             c, n = units[k]
             h_scaled[k] = work.tile([P, PACK * P, PACK], F32, name="h_scaled")
             for pair in range(PACK // 2):
-                ht_ps = psum_tr.tile([P, 2, 2 * P], F32, tag="tr")
+                ht_ps = psum.tile([P, 2, 2 * P], F32, tag="bank")
                 for r in range(2):
                     h_words = h_raw[n][:, c, 2 * pair + r, :].bitcast(F32)
                     for u in range(2):
@@ -176,7 +184,7 @@ def tile_llamamlp_halfwaygin_pa_kernel(tc, h_inter, adjacency, Wd, eps, alpha, o
             c, n = units[k]
             g_grouped[k] = work.tile([P, PACK * P, PACK], BF16, name="g_grouped", align_bytes=64)
             for ti in range(PACK):
-                agg_ps = psum_acc.tile([P, PACK, P], F32, tag="acc")
+                agg_ps = psum.tile([P, PACK, P], F32, tag="bank")
                 for tf in range(PACK):
                     for cp in range(BLOCKS):
                         f_cols = slice(HD * cp + P * tf, HD * cp + P * (tf + 1))
@@ -210,10 +218,7 @@ def tile_llamamlp_halfwaygin_pa_kernel(tc, h_inter, adjacency, Wd, eps, alpha, o
         def project(q, copies):
             for c in range(BLOCKS):
                 for u in range(2):
-                    if u == 0:
-                        out_ps = psum_tr.tile([P, 2, CHUNK], F32, tag="tr")
-                    else:
-                        out_ps = psum_acc.tile([P, 2, CHUNK], F32, tag="acc")
+                    out_ps = psum.tile([P, 2, CHUNK], F32, tag="bank")
                     for e in range(2):
                         i_cols = slice(P * (2 * u + e), P * (2 * u + e + 1))
                         for n in range(HEADS):
@@ -246,11 +251,11 @@ def tile_llamamlp_halfwaygin_pa_kernel(tc, h_inter, adjacency, Wd, eps, alpha, o
         load_h(2)
 
         transpose_adjacency(0, (0, 1))
-        regroup_h(0, 0, vcopy, scopy)
+        regroup_h(0, 0)
         quantise_adjacency(0, (0,))
         nc.vector.tensor_scalar_add(out=one_plus_eps[:], in0=eps_bf[:], scalar1=1.0)
         nc.vector.tensor_copy(out=alpha_f[:], in_=alpha_bf[:])
-        regroup_h(0, 1, vcopy, scopy)
+        regroup_h(0, 1)
         quantise_h(0, 0)
         quantise_adjacency(0, (1,))
         quantise_h(0, 1)
@@ -268,19 +273,18 @@ def tile_llamamlp_halfwaygin_pa_kernel(tc, h_inter, adjacency, Wd, eps, alpha, o
                     load_h(3)
                 load_adjacency(k + A_BUFS)
                 load_wd(k)
+            if k > 0 and (k - 1) // BLOCKS + 1 < HEADS:
+                quantise_h((k - 1) // BLOCKS + 1, (k - 1) % BLOCKS)
             if last - HEADS <= k < last:
                 regroup_wd(0, k - (last - HEADS), vcopy)
             if next_head < HEADS:
-                regroup_h(next_head, k % BLOCKS, vcopy, scopy)
+                regroup_h(next_head, k % BLOCKS)
             if k == last:
+                quantise_wd(0)
                 for n in range(HEADS):
                     regroup_wd(1, n, scopy)
             if k > 0:
-                if (k - 1) // BLOCKS + 1 < HEADS:
-                    quantise_h((k - 1) // BLOCKS + 1, (k - 1) % BLOCKS)
                 quantise_g(k - 1)
-            if k == last:
-                quantise_wd(0)
             if k < last:
                 quantise_adjacency(k + 1, all_tiles)
             mix(k)

@@ -98,22 +98,24 @@ def tile_llamamlp_halfwaygin_pa_kernel(tc, h_inter, adjacency, Wd, eps, alpha, o
                 out=wd_raw[n][:].rearrange("p (u e) d -> p u (e d)", u=2), in_=wd_view[n, :, :, :]
             )
 
-        def regroup_h(n, c):
+        def regroup_h(n, c, tensor_parity=(1,)):
             if c == 0:
                 h_grouped[n] = work.tile(
                     [P, BLOCKS, HD, PACK], BF16, name="h_grouped", tag="grouped", bufs=GROUPED_BUFS, align_bytes=64
                 )
             dst = h_grouped[n][:, c, :, :].rearrange("p (u e q) t -> p e u q t", u=2, e=2)
             src = h_raw[n][:, c, :, :].rearrange("p t (u q e) -> p e u q t", u=2, e=2)
-            nc.vector.tensor_copy(out=dst[:, 0, :, :, :], in_=src[:, 0, :, :, :])
-            odd_ps = psum.tile([P, 2, P, PACK], BF16, tag="bank")
-            for u in range(2):
-                nc.tensor.matmul(odd_ps[:, u, :, :], ident_bf[:], src[:, 1, u, :, :], start=True, stop=True)
             words = h_grouped[n][:, c, :, :].rearrange("p x t -> p (x t)").bitcast(F32)
-            nc.scalar.copy(
-                out=words.rearrange("p (u e w) -> p e u w", u=2, e=2)[:, 1, :, :],
-                in_=odd_ps[:].rearrange("p u q t -> p (u q t)").bitcast(F32).rearrange("p (u w) -> p u w", u=2),
-            )
+            words = words.rearrange("p (u e w) -> p e u w", u=2, e=2)
+            for e in range(2):
+                if e not in tensor_parity:
+                    nc.vector.tensor_copy(out=dst[:, e, :, :, :], in_=src[:, e, :, :, :])
+                    continue
+                turned = psum.tile([P, 2, P, PACK], BF16, tag="bank")
+                for u in range(2):
+                    nc.tensor.matmul(turned[:, u, :, :], ident_bf[:], src[:, e, u, :, :], start=True, stop=True)
+                turned_words = turned[:].rearrange("p u q t -> p (u q t)").bitcast(F32)
+                nc.scalar.copy(out=words[:, e, :, :], in_=turned_words.rearrange("p (u w) -> p u w", u=2))
 
         def quantise_h(n, c):
             cols = slice(HD * c, HD * (c + 1))
@@ -123,15 +125,27 @@ def tile_llamamlp_halfwaygin_pa_kernel(tc, h_inter, adjacency, Wd, eps, alpha, o
                 in_=h_grouped[n][:, c, :, :].rearrange("p x t -> p (x t)"),
             )
 
-        def regroup_wd(q, n, copy):
+        def regroup_wd(q, n, way):
             if n == 0:
                 wd_grouped[q] = work.tile(
                     [P, HEADS, CHUNK, PACK], BF16, name="wd_grouped", tag="grouped", bufs=GROUPED_BUFS, align_bytes=64
                 )
-            copy(
-                out=wd_grouped[q][:, n, :, :].rearrange("p (x i) t -> p x t i", i=4),
-                in_=wd_raw[n][:, :, CHUNK * q : CHUNK * (q + 1)].rearrange("p t (x i) -> p x t i", i=4),
-            )
+            dst = wd_grouped[q][:, n, :, :]
+            src = wd_raw[n][:, :, CHUNK * q : CHUNK * (q + 1)]
+            if way == "tensor":
+                turned = psum.tile([P, CHUNK, PACK], BF16, tag="bank")
+                for x in range(0, CHUNK, P):
+                    rows = src[:, :, x : x + P].rearrange("p t x -> p x t")
+                    nc.tensor.matmul(turned[:, x : x + P, :], ident_bf[:], rows, start=True, stop=True)
+                nc.scalar.copy(
+                    out=dst.rearrange("p x t -> p (x t)").bitcast(F32),
+                    in_=turned[:].rearrange("p x t -> p (x t)").bitcast(F32),
+                )
+            else:
+                copy = nc.vector.tensor_copy if way == "vector" else nc.scalar.copy
+                copy(
+                    out=dst.rearrange("p (x i) t -> p x t i", i=4), in_=src.rearrange("p t (x i) -> p x t i", i=4)
+                )
 
         def quantise_wd(q):
             nc.vector.quantize_mx(
@@ -140,7 +154,7 @@ def tile_llamamlp_halfwaygin_pa_kernel(tc, h_inter, adjacency, Wd, eps, alpha, o
                 in_=wd_grouped[q][:].rearrange("p n x t -> p (n x t)"),
             )
 
-        def transpose_adjacency(k, tiles):
+        def transpose_adjacency(k, tiles, copies=(nc.scalar.copy,)):
             for ti in tiles:
                 a_words = a_raw[k][:, ti, :].bitcast(F32)
                 at_ps = psum.tile([P, BLOCKS, 2, P], F32, tag="bank")
@@ -149,9 +163,8 @@ def tile_llamamlp_halfwaygin_pa_kernel(tc, h_inter, adjacency, Wd, eps, alpha, o
                         w0 = (2 * c + u) * P
                         nc.tensor.transpose(at_ps[:, c, u, :], a_words[:, w0 : w0 + P], ident[:])
                 a_grouped[(k, ti)] = work.tile([P, BLOCKS, P, PACK], BF16, name="a_grouped", bufs=PACK, align_bytes=64)
-                nc.scalar.copy(
-                    out=a_grouped[(k, ti)][:].bitcast(F32), in_=at_ps[:].rearrange("p c u i -> p c i u")
-                )
+                copy = copies[ti % len(copies)]
+                copy(out=a_grouped[(k, ti)][:].bitcast(F32), in_=at_ps[:].rearrange("p c u i -> p c i u"))
 
         def quantise_adjacency(k, tiles):
             if tiles[0] == 0:
@@ -215,16 +228,16 @@ def tile_llamamlp_halfwaygin_pa_kernel(tc, h_inter, adjacency, Wd, eps, alpha, o
                 in_=g_grouped[k][:].rearrange("p x t -> p (x t)"),
             )
 
-        def project(q, copies):
-            for c in range(BLOCKS):
-                for u in range(2):
-                    out_ps = psum.tile([P, 2, CHUNK], F32, tag="bank")
-                    for e in range(2):
+        def project(q, c, copies, split=False):
+            for u in range(2):
+                for es in ((0,), (1,)) if split else ((0, 1),):
+                    out_ps = psum.tile([P, len(es), CHUNK], F32, tag="bank")
+                    for e in es:
                         i_cols = slice(P * (2 * u + e), P * (2 * u + e + 1))
                         for n in range(HEADS):
                             d_cols = slice(CHUNK * n, CHUNK * (n + 1))
                             nc.tensor.matmul_mx(
-                                out=out_ps[:, e, :],
+                                out=out_ps[:, e - es[0], :],
                                 lhsT=g_codes[:, n, c, i_cols].bitcast(FP8X4),
                                 lhsT_scale=g_scales[:, n, c, i_cols],
                                 rhs=wd_codes[:, q, d_cols].bitcast(FP8X4),
@@ -232,69 +245,72 @@ def tile_llamamlp_halfwaygin_pa_kernel(tc, h_inter, adjacency, Wd, eps, alpha, o
                                 start=(n == 0),
                                 stop=(n == HEADS - 1),
                             )
-                    out_sb = work.tile([P, 2, CHUNK], F32, bufs=4)
-                    copies[u](out=out_sb[:], in_=out_ps[:])
-                    nc.sync.dma_start(out=out_view[c, u, :, :, CHUNK * q : CHUNK * (q + 1)], in_=out_sb[:])
+                    out_sb = work.tile([P, len(es), CHUNK], F32, name="out_sb", bufs=6)
+                    copies[(u + es[0]) % 2](out=out_sb[:], in_=out_ps[:])
+                    nc.sync.dma_start(
+                        out=out_view[c, u, :, es[0] : es[-1] + 1, CHUNK * q : CHUNK * (q + 1)], in_=out_sb[:]
+                    )
 
         vcopy = nc.vector.tensor_copy
         scopy = nc.scalar.copy
         last = len(units) - 1
         all_tiles = range(PACK)
 
-        load_adjacency(0, (0,))
+        load_adjacency(0)
         load_h(0)
-        load_adjacency(0, (1,))
         load_adjacency(1)
         load_h(1)
         load_adjacency(2)
         load_adjacency(3)
         load_h(2)
 
-        transpose_adjacency(0, (0, 1))
-        regroup_h(0, 0)
-        quantise_adjacency(0, (0,))
+        transpose_adjacency(0, all_tiles)
+        quantise_adjacency(0, (0, 1))
+        regroup_h(0, 0, ())
         nc.vector.tensor_scalar_add(out=one_plus_eps[:], in0=eps_bf[:], scalar1=1.0)
         nc.vector.tensor_copy(out=alpha_f[:], in_=alpha_bf[:])
         regroup_h(0, 1)
-        quantise_h(0, 0)
-        quantise_adjacency(0, (1,))
-        quantise_h(0, 1)
-        transpose_adjacency(0, (2, 3))
         transpose_h(0)
+        quantise_h(0, 0)
         quantise_adjacency(0, (2, 3))
+        quantise_h(0, 1)
 
         for k in range(last + 1):
             next_head = k // BLOCKS + 1
             if k < last:
-                transpose_adjacency(k + 1, all_tiles)
+                transpose_adjacency(k + 1, all_tiles, (scopy, vcopy) if k == 0 else (scopy,))
                 transpose_h(k + 1)
-            if k + 1 + A_BUFS <= last + 1:
+            if k + A_BUFS <= last:
                 if k == 1:
                     load_h(3)
                 load_adjacency(k + A_BUFS)
                 load_wd(k)
             if k > 0 and (k - 1) // BLOCKS + 1 < HEADS:
                 quantise_h((k - 1) // BLOCKS + 1, (k - 1) % BLOCKS)
-            if last - HEADS <= k < last:
-                regroup_wd(0, k - (last - HEADS), vcopy)
             if next_head < HEADS:
                 regroup_h(next_head, k % BLOCKS)
+            if last - HEADS <= k < last:
+                regroup_wd(0, k - (last - HEADS), "tensor" if k % 2 else "vector")
             if k == last:
                 quantise_wd(0)
-                for n in range(HEADS):
-                    regroup_wd(1, n, scopy)
+                for n in range(3):
+                    regroup_wd(1, n, "scalar")
             if k > 0:
                 quantise_g(k - 1)
             if k < last:
                 quantise_adjacency(k + 1, all_tiles)
             mix(k)
-        regroup_wd(2, 0, vcopy)
+        project(0, 0, (scopy, scopy))
         quantise_g(last)
+        for n in range(3, HEADS):
+            regroup_wd(1, n, "vector")
         quantise_wd(1)
+        project(0, 1, (scopy, scopy))
 
-        for q in range(CHUNKS):
-            if 2 <= q + 1 < CHUNKS:
-                for n in range(1 if q == 1 else 0, HEADS):
-                    regroup_wd(q + 1, n, vcopy)
+        for q in range(1, CHUNKS):
+            if q + 1 < CHUNKS:
+                for n in range(HEADS):
+                    regroup_wd(q + 1, n, "vector")
                 quantise_wd(q + 1)
-            project(q, (scopy, vcopy if q == CHUNKS - 1 else scopy))
+            for c in range(BLOCKS):
+                project(q, c, (scopy, vcopy if q == CHUNKS - 1 else scopy), split=(q == CHUNKS - 1 and c == BLOCKS - 1))

@@ -57,6 +57,7 @@ def tile_llamamlp_halfwaygin_pa_kernel(tc, h_inter, adjacency, Wd, eps, alpha, o
         nc.vector.memset(warm[:], 0.0)
         warm_out = keep.tile([P, 8], F32, name="warm_out")
         nc.scalar.copy(out=warm_out[:], in_=warm[:])
+        nc.vector.tensor_scalar_add(out=one_plus_eps[:], in0=eps_bf[:], scalar1=1.0)
 
         h_raw = [keep.tile([P, BLOCKS, PACK, HD], BF16, name="h_raw%d" % n) for n in range(HEADS)]
         wd_raw = [keep.tile([P, PACK, D], BF16, name="wd_raw%d" % n) for n in range(HEADS)]
@@ -76,8 +77,8 @@ def tile_llamamlp_halfwaygin_pa_kernel(tc, h_inter, adjacency, Wd, eps, alpha, o
         g_grouped = {}
         wd_grouped = {}
 
-        def load_h(n):
-            for c in range(BLOCKS):
+        def load_h(n, blocks=range(BLOCKS)):
+            for c in blocks:
                 for u in range(2):
                     nc.sync.dma_start(
                         out=h_raw[n][:, c, 2 * u : 2 * u + 2, :],
@@ -256,30 +257,31 @@ def tile_llamamlp_halfwaygin_pa_kernel(tc, h_inter, adjacency, Wd, eps, alpha, o
         last = len(units) - 1
         all_tiles = range(PACK)
 
-        load_adjacency(0)
-        load_h(0)
+        load_h(0, (0,))
+        load_adjacency(0, (0,))
+        load_h(0, (1,))
+        load_adjacency(0, (1,))
         load_adjacency(1)
         load_h(1)
         load_adjacency(2)
         load_adjacency(3)
         load_h(2)
 
-        transpose_adjacency(0, all_tiles)
-        quantise_adjacency(0, (0, 1))
-        regroup_h(0, 0, ())
-        nc.vector.tensor_scalar_add(out=one_plus_eps[:], in0=eps_bf[:], scalar1=1.0)
-        nc.vector.tensor_copy(out=alpha_f[:], in_=alpha_bf[:])
-        regroup_h(0, 1)
         transpose_h(0)
+        regroup_h(0, 0, ())
+        transpose_adjacency(0, (0, 1))
+        nc.vector.tensor_copy(out=alpha_f[:], in_=alpha_bf[:])
         quantise_h(0, 0)
+        quantise_adjacency(0, (0, 1))
+        regroup_h(0, 1)
+        transpose_adjacency(0, (2, 3))
         quantise_adjacency(0, (2, 3))
         quantise_h(0, 1)
 
         for k in range(last + 1):
             next_head = k // BLOCKS + 1
             if k < last:
-                transpose_adjacency(k + 1, all_tiles, (scopy, vcopy) if k == 0 else (scopy,))
-                transpose_h(k + 1)
+                transpose_adjacency(k + 1, all_tiles)
             if k + A_BUFS <= last:
                 if k == 1:
                     load_h(3)
@@ -290,7 +292,9 @@ def tile_llamamlp_halfwaygin_pa_kernel(tc, h_inter, adjacency, Wd, eps, alpha, o
             if next_head < HEADS:
                 regroup_h(next_head, k % BLOCKS)
             if last - HEADS <= k < last:
-                regroup_wd(0, k - (last - HEADS), "tensor" if k % 2 else "vector")
+                regroup_wd(0, k - (last - HEADS), "vector" if k in (4, ) else "tensor")
+            if k < last:
+                transpose_h(k + 1)
             if k == last:
                 quantise_wd(0)
                 for n in range(3):

@@ -53,10 +53,10 @@ def tile_llamamlp_halfwaygin_pa_kernel(tc, h_inter, adjacency, Wd, eps, alpha, o
         nc.scalar.dma_start(out=alpha_bf[:], in_=alpha.partition_broadcast(P))
         one_plus_eps = keep.tile([P, HEADS], F32, name="one_plus_eps")
         alpha_f = keep.tile([P, HEADS], F32, name="alpha_f")
-        warm = keep.tile([P, 8], F32, name="warm")
-        nc.vector.memset(warm[:], 0.0)
-        warm_out = keep.tile([P, 8], F32, name="warm_out")
-        nc.scalar.copy(out=warm_out[:], in_=warm[:])
+        zeros = keep.tile([P, K_PASS], BF16, name="zeros")
+        nc.vector.memset(zeros[:], 0.0)
+        unused = keep.tile([P, 16], BF16, name="unused")
+        nc.scalar.copy(out=unused[:], in_=zeros[:, 0:16])
         nc.vector.tensor_scalar_add(out=one_plus_eps[:], in0=eps_bf[:], scalar1=1.0)
 
         h_raw = [keep.tile([P, BLOCKS, PACK, HD], BF16, name="h_raw%d" % n) for n in range(HEADS)]
@@ -67,6 +67,11 @@ def tile_llamamlp_halfwaygin_pa_kernel(tc, h_inter, adjacency, Wd, eps, alpha, o
         wd_scales = keep.tile([P, CHUNKS, HEADS * CHUNK], U8, name="wd_scales", align_bytes=64)
         g_codes = keep.tile([P, HEADS, BLOCKS, K_PASS], U32, name="g_codes", align_bytes=64)
         g_scales = keep.tile([P, HEADS, BLOCKS, K_PASS], U8, name="g_scales", align_bytes=64)
+
+        def keep_clock(passes):
+            idle = psum.tile([P, K_PASS], F32, tag="bank")
+            for i in range(passes):
+                nc.tensor.matmul(idle[:], zeros[:, :P], zeros[:], start=True, stop=True)
 
         a_raw = {}
         a_grouped = {}
@@ -99,24 +104,39 @@ def tile_llamamlp_halfwaygin_pa_kernel(tc, h_inter, adjacency, Wd, eps, alpha, o
                 out=wd_raw[n][:].rearrange("p (u e) d -> p u (e d)", u=2), in_=wd_view[n, :, :, :]
             )
 
-        def regroup_h(n, c, tensor_parity=(1,)):
-            if c == 0:
+        def grouped_h(n, c, e):
+            if n not in h_grouped:
                 h_grouped[n] = work.tile(
                     [P, BLOCKS, HD, PACK], BF16, name="h_grouped", tag="grouped", bufs=GROUPED_BUFS, align_bytes=64
                 )
-            dst = h_grouped[n][:, c, :, :].rearrange("p (u e q) t -> p e u q t", u=2, e=2)
-            src = h_raw[n][:, c, :, :].rearrange("p t (u q e) -> p e u q t", u=2, e=2)
-            words = h_grouped[n][:, c, :, :].rearrange("p x t -> p (x t)").bitcast(F32)
-            words = words.rearrange("p (u e w) -> p e u w", u=2, e=2)
-            for e in range(2):
-                if e not in tensor_parity:
-                    nc.vector.tensor_copy(out=dst[:, e, :, :, :], in_=src[:, e, :, :, :])
-                    continue
-                turned = psum.tile([P, 2, P, PACK], BF16, tag="bank")
-                for u in range(2):
-                    nc.tensor.matmul(turned[:, u, :, :], ident_bf[:], src[:, e, u, :, :], start=True, stop=True)
-                turned_words = turned[:].rearrange("p u q t -> p (u q t)").bitcast(F32)
-                nc.scalar.copy(out=words[:, e, :, :], in_=turned_words.rearrange("p (u w) -> p u w", u=2))
+            return h_grouped[n][:, c, :, :].rearrange("p (u e q) t -> p e u q t", u=2, e=2)[:, e, :, :, :]
+
+        def features(n, c, e):
+            return h_raw[n][:, c, :, :].rearrange("p t (u q e) -> p e u q t", u=2, e=2)[:, e, :, :, :]
+
+        def regroup_h_vector(n, c, e, us=slice(0, 2)):
+            nc.vector.tensor_copy(out=grouped_h(n, c, e)[:, us, :, :], in_=features(n, c, e)[:, us, :, :])
+
+        def regroup_h_gpsimd(n, c, e, us=slice(0, 2)):
+            dst = grouped_h(n, c, e)[:, us, :, :]
+            src = features(n, c, e)[:, us, :, :]
+            nc.vector.tensor_copy(out=dst[:, 0, 0:8, :], in_=src[:, 0, 0:8, :])
+            nc.gpsimd.tensor_scalar(out=dst, in0=src, scalar1=1.0, scalar2=0.0, op0=ALU.mult, op1=ALU.add)
+
+        def regroup_h_scalar(n, c, e, us):
+            nc.scalar.copy(out=grouped_h(n, c, e)[:, us, :, :], in_=features(n, c, e)[:, us, :, :])
+
+        def regroup_h_tensor(n, c, e, us=slice(0, 2)):
+            dst = grouped_h(n, c, e)[:, us, :, :]
+            src = features(n, c, e)[:, us, :, :]
+            halves = us.stop - us.start
+            turned = psum.tile([P, halves, P, PACK], BF16, tag="bank")
+            for u in range(halves):
+                nc.tensor.matmul(turned[:, u, :, :], ident_bf[:], src[:, u, :, :], start=True, stop=True)
+            nc.scalar.copy(
+                out=dst.rearrange("p u q t -> p u (q t)").bitcast(F32),
+                in_=turned[:].rearrange("p u q t -> p u (q t)").bitcast(F32),
+            )
 
         def quantise_h(n, c):
             cols = slice(HD * c, HD * (c + 1))
@@ -133,7 +153,11 @@ def tile_llamamlp_halfwaygin_pa_kernel(tc, h_inter, adjacency, Wd, eps, alpha, o
                 )
             dst = wd_grouped[q][:, n, :, :]
             src = wd_raw[n][:, :, CHUNK * q : CHUNK * (q + 1)]
-            if way == "tensor":
+            if way == "gpsimd":
+                src4 = src.rearrange("p t x -> p x t")
+                nc.vector.tensor_copy(out=dst[:, 0:8, :], in_=src4[:, 0:8, :])
+                nc.gpsimd.tensor_scalar(out=dst, in0=src4, scalar1=1.0, scalar2=0.0, op0=ALU.mult, op1=ALU.add)
+            elif way == "tensor":
                 turned = psum.tile([P, CHUNK, PACK], BF16, tag="bank")
                 for x in range(0, CHUNK, P):
                     rows = src[:, :, x : x + P].rearrange("p t x -> p x t")
@@ -194,10 +218,11 @@ def tile_llamamlp_halfwaygin_pa_kernel(tc, h_inter, adjacency, Wd, eps, alpha, o
                     scale=one_plus_eps[:, n : n + 1],
                 )
 
-        def mix(k):
+        def mix(k, tiles):
             c, n = units[k]
-            g_grouped[k] = work.tile([P, PACK * P, PACK], BF16, name="g_grouped", align_bytes=64)
-            for ti in range(PACK):
+            if tiles[0] == 0:
+                g_grouped[k] = work.tile([P, PACK * P, PACK], BF16, name="g_grouped", align_bytes=64)
+            for ti in tiles:
                 agg_ps = psum.tile([P, PACK, P], F32, tag="bank")
                 for tf in range(PACK):
                     for cp in range(BLOCKS):
@@ -256,6 +281,7 @@ def tile_llamamlp_halfwaygin_pa_kernel(tc, h_inter, adjacency, Wd, eps, alpha, o
         scopy = nc.scalar.copy
         last = len(units) - 1
         all_tiles = range(PACK)
+        h_parts = {0: [(1, 0), (1, 1)], 1: [(2, 0)], 2: [(2, 1)], 3: [(3, 0)], 4: [(3, 1)]};
 
         load_h(0, (0,))
         load_adjacency(0, (0,))
@@ -264,37 +290,42 @@ def tile_llamamlp_halfwaygin_pa_kernel(tc, h_inter, adjacency, Wd, eps, alpha, o
         load_adjacency(1)
         load_h(1)
         load_adjacency(2)
-        load_adjacency(3)
         load_h(2)
+        load_adjacency(3)
 
+        keep_clock(6)
         transpose_h(0)
-        regroup_h(0, 0, ())
+        regroup_h_vector(0, 0, 0)
+        regroup_h_vector(0, 0, 1)
         transpose_adjacency(0, (0, 1))
         nc.vector.tensor_copy(out=alpha_f[:], in_=alpha_bf[:])
         quantise_h(0, 0)
         quantise_adjacency(0, (0, 1))
-        regroup_h(0, 1)
+        regroup_h_vector(0, 1, 0)
+        regroup_h_tensor(0, 1, 1)
         transpose_adjacency(0, (2, 3))
         quantise_adjacency(0, (2, 3))
         quantise_h(0, 1)
+        keep_clock(2)
 
         for k in range(last + 1):
-            next_head = k // BLOCKS + 1
             if k < last:
                 transpose_adjacency(k + 1, all_tiles)
+            if k < last:
+                transpose_h(k + 1)
             if k + A_BUFS <= last:
                 if k == 1:
                     load_h(3)
                 load_adjacency(k + A_BUFS)
                 load_wd(k)
-            if k > 0 and (k - 1) // BLOCKS + 1 < HEADS:
-                quantise_h((k - 1) // BLOCKS + 1, (k - 1) % BLOCKS)
-            if next_head < HEADS:
-                regroup_h(next_head, k % BLOCKS)
-            if last - HEADS <= k < last:
-                regroup_wd(0, k - (last - HEADS), "vector" if k in (4, ) else "tensor")
-            if k < last:
-                transpose_h(k + 1)
+            for head, block in h_parts.get(k - 1, []):
+                quantise_h(head, block)
+            for head, block in h_parts.get(k, []):
+                if k == 0:
+                    continue
+                regroup_h_scalar(head, block, 1, slice(0, 1))
+            if k in (3, 4):
+                regroup_wd(0, k - 3, "vector")
             if k == last:
                 quantise_wd(0)
                 for n in range(3):
@@ -303,7 +334,19 @@ def tile_llamamlp_halfwaygin_pa_kernel(tc, h_inter, adjacency, Wd, eps, alpha, o
                 quantise_g(k - 1)
             if k < last:
                 quantise_adjacency(k + 1, all_tiles)
-            mix(k)
+            if k > 0:
+                for head, block in h_parts.get(k, []):
+                    regroup_h_gpsimd(head, block, 0)
+                    regroup_h_gpsimd(head, block, 1, slice(1, 2))
+            if k in (5, 6):
+                regroup_wd(0, k - 3, "gpsimd")
+            if k == 0:
+                regroup_h_vector(1, 0, 0)
+                regroup_h_vector(1, 0, 1)
+                regroup_h_gpsimd(1, 1, 0)
+            mix(k, all_tiles)
+            if k == 0:
+                regroup_h_vector(1, 1, 1)
         project(0, 0, (scopy, scopy))
         quantise_g(last)
         for n in range(3, HEADS):

@@ -32,7 +32,7 @@ def tile_llamamlp_halfwaygin_pa_kernel(tc, h_inter, adjacency, Wd, eps, alpha, o
 
     h_view = h_inter.rearrange("b (c u p e) f -> (b c) u p e f", c=BLOCKS, u=2, p=P, e=2)
     a_view = adjacency.rearrange("b n (c u p e) j -> (b n) c p u (e j)", c=BLOCKS, u=2, p=P, e=2)
-    wd_view = Wd.rearrange("(n u p e) d -> n p u (e d)", n=HEADS, u=2, p=P, e=2)
+    wd_view = Wd.rearrange("(n u p e) d -> n u p e d", n=HEADS, u=2, p=P, e=2)
     out_view = out.rearrange("b (c u p e) d -> (b c) u p e d", c=BLOCKS, u=2, p=P, e=2)
 
     units = [(c, n) for n in range(HEADS) for c in range(BLOCKS)]
@@ -99,10 +99,10 @@ def tile_llamamlp_halfwaygin_pa_kernel(tc, h_inter, adjacency, Wd, eps, alpha, o
                     out=a_raw[k][:, 2 * u : 2 * u + 2, :].rearrange("p e j -> p (e j)"), in_=a_view[n, c, :, u, :]
                 )
 
-        def load_wd(n):
-            nc.sync.dma_start(
-                out=wd_raw[n][:].rearrange("p (u e) d -> p u (e d)", u=2), in_=wd_view[n, :, :, :]
-            )
+        def load_wd(n, half):
+            cols = slice(D // 2 * half, D // 2 * (half + 1))
+            for u in range(2):
+                nc.sync.dma_start(out=wd_raw[n][:, 2 * u : 2 * u + 2, cols], in_=wd_view[n, u, :, :, cols])
 
         def grouped_h(n, c, e):
             if n not in h_grouped:
@@ -290,8 +290,9 @@ def tile_llamamlp_halfwaygin_pa_kernel(tc, h_inter, adjacency, Wd, eps, alpha, o
         load_adjacency(1)
         load_h(1)
         load_adjacency(2)
-        load_h(2)
+        load_h(2, (0,))
         load_adjacency(3)
+        load_h(2, (1,))
 
         keep_clock(6)
         transpose_h(0)
@@ -304,20 +305,22 @@ def tile_llamamlp_halfwaygin_pa_kernel(tc, h_inter, adjacency, Wd, eps, alpha, o
         regroup_h_vector(0, 1, 0)
         regroup_h_tensor(0, 1, 1)
         transpose_adjacency(0, (2, 3))
-        quantise_adjacency(0, (2, 3))
         quantise_h(0, 1)
+        quantise_adjacency(0, (2, 3))
         keep_clock(2)
 
         for k in range(last + 1):
             if k < last:
                 transpose_adjacency(k + 1, all_tiles)
-            if k < last:
                 transpose_h(k + 1)
             if k + A_BUFS <= last:
-                if k == 1:
-                    load_h(3)
                 load_adjacency(k + A_BUFS)
-                load_wd(k)
+                if k < BLOCKS:
+                    load_h(3, (k,))
+                load_wd(k, 0)
+                if k + A_BUFS == last:
+                    for n in range(HEADS):
+                        load_wd(n, 1)
             for head, block in h_parts.get(k - 1, []):
                 quantise_h(head, block)
             for head, block in h_parts.get(k, []):
@@ -325,7 +328,7 @@ def tile_llamamlp_halfwaygin_pa_kernel(tc, h_inter, adjacency, Wd, eps, alpha, o
                     continue
                 regroup_h_scalar(head, block, 1, slice(0, 1))
             if k in (3, 4):
-                regroup_wd(0, k - 3, "vector")
+                regroup_wd(0, k - 3, "tensor")
             if k == last:
                 quantise_wd(0)
                 for n in range(3):

@@ -117,10 +117,11 @@ def tile_llamamlp_halfwaygin_pa_kernel(tc, h_inter, adjacency, Wd, eps, alpha, o
         def regroup_h_vector(n, c, e, us=slice(0, 2)):
             nc.vector.tensor_copy(out=grouped_h(n, c, e)[:, us, :, :], in_=features(n, c, e)[:, us, :, :])
 
-        def regroup_h_gpsimd(n, c, e, us=slice(0, 2)):
+        def regroup_h_gpsimd(n, c, e, us=slice(0, 2), hold=True):
             dst = grouped_h(n, c, e)[:, us, :, :]
             src = features(n, c, e)[:, us, :, :]
-            nc.vector.tensor_copy(out=dst[:, 0, 0:8, :], in_=src[:, 0, 0:8, :])
+            if hold:
+                nc.vector.tensor_copy(out=dst[:, 0, 0:8, :], in_=src[:, 0, 0:8, :])
             nc.gpsimd.tensor_scalar(out=dst, in0=src, scalar1=1.0, scalar2=0.0, op0=ALU.mult, op1=ALU.add)
 
         def regroup_h_scalar(n, c, e, us):
@@ -187,19 +188,24 @@ def tile_llamamlp_halfwaygin_pa_kernel(tc, h_inter, adjacency, Wd, eps, alpha, o
                     for u in range(2):
                         w0 = (2 * c + u) * P
                         nc.tensor.transpose(at_ps[:, c, u, :], a_words[:, w0 : w0 + P], ident[:])
-                a_grouped[(k, ti)] = work.tile([P, BLOCKS, P, PACK], BF16, name="a_grouped", bufs=PACK, align_bytes=64)
+                if ti % 2 == 0:
+                    a_grouped[(k, ti // 2)] = work.tile([P, 2, BLOCKS, P, PACK], BF16, name="a_grouped", align_bytes=64)
                 copy = copies[ti % len(copies)]
-                copy(out=a_grouped[(k, ti)][:].bitcast(F32), in_=at_ps[:].rearrange("p c u i -> p c i u"))
+                copy(
+                    out=a_grouped[(k, ti // 2)][:, ti % 2, :, :, :].bitcast(F32),
+                    in_=at_ps[:].rearrange("p c u i -> p c i u"),
+                )
 
-        def quantise_adjacency(k, tiles):
+        def quantise_adjacency(k, tiles, width=1):
             if tiles[0] == 0:
                 a_codes[k] = work.tile([P, PACK, BLOCKS * P], U32, name="a_codes", align_bytes=64)
                 a_scales[k] = work.tile([P, PACK, BLOCKS * P], U8, name="a_scales", align_bytes=64)
-            for ti in tiles:
+            for ti in range(tiles[0], tiles[-1] + 1, width):
+                part = slice(ti % 2, ti % 2 + width)
                 nc.vector.quantize_mx(
-                    out=a_codes[k][:, ti, :].bitcast(FP8X4),
-                    scales=a_scales[k][:, ti, :],
-                    in_=a_grouped[(k, ti)][:].rearrange("p c i t -> p (c i t)"),
+                    out=a_codes[k][:, ti : ti + width, :].rearrange("p t x -> p (t x)").bitcast(FP8X4),
+                    scales=a_scales[k][:, ti : ti + width, :].rearrange("p t x -> p (t x)"),
+                    in_=a_grouped[(k, ti // 2)][:, part, :, :, :].rearrange("p t c i e -> p (t c i e)"),
                 )
 
         def transpose_h(k):
@@ -340,27 +346,28 @@ def tile_llamamlp_halfwaygin_pa_kernel(tc, h_inter, adjacency, Wd, eps, alpha, o
             if k > 0:
                 for head, block in h_parts.get(k, []):
                     regroup_h_gpsimd(head, block, 0)
-                    regroup_h_gpsimd(head, block, 1, slice(1, 2))
+                    regroup_h_gpsimd(head, block, 1, slice(1, 2), hold=False)
             if k in (5, 6):
                 regroup_wd(0, k - 3, "gpsimd")
+            if k == last:
+                regroup_wd(1, 3, "gpsimd")
             if k == 0:
-                regroup_h_vector(1, 0, 0)
-                regroup_h_vector(1, 0, 1)
-                regroup_h_gpsimd(1, 1, 0)
+                regroup_h_gpsimd(1, 0, 0)
+                regroup_h_gpsimd(1, 0, 1, slice(0, 1), hold=False)
             mix(k, all_tiles)
             if k == 0:
+                regroup_h_vector(1, 0, 1, slice(1, 2))
+                regroup_h_vector(1, 1, 0)
                 regroup_h_vector(1, 1, 1)
         project(0, 0, (scopy, scopy))
         quantise_g(last)
-        for n in range(3, HEADS):
-            regroup_wd(1, n, "vector")
         quantise_wd(1)
         project(0, 1, (scopy, scopy))
 
         for q in range(1, CHUNKS):
             if q + 1 < CHUNKS:
                 for n in range(HEADS):
-                    regroup_wd(q + 1, n, "vector")
+                    regroup_wd(q + 1, n, "scalar" if n == 0 else "vector")
                 quantise_wd(q + 1)
             for c in range(BLOCKS):
                 project(q, c, (scopy, vcopy if q == CHUNKS - 1 else scopy), split=(q == CHUNKS - 1 and c == BLOCKS - 1))

@@ -57,7 +57,6 @@ def tile_llamamlp_halfwaygin_pa_kernel(tc, h_inter, adjacency, Wd, eps, alpha, o
         nc.vector.memset(zeros[:], 0.0)
         unused = keep.tile([P, 16], BF16, name="unused")
         nc.scalar.copy(out=unused[:], in_=zeros[:, 0:16])
-        nc.vector.tensor_scalar_add(out=one_plus_eps[:], in0=eps_bf[:], scalar1=1.0)
 
         h_raw = [keep.tile([P, BLOCKS, PACK, HD], BF16, name="h_raw%d" % n) for n in range(HEADS)]
         wd_raw = [keep.tile([P, PACK, D], BF16, name="wd_raw%d" % n) for n in range(HEADS)]
@@ -90,14 +89,18 @@ def tile_llamamlp_halfwaygin_pa_kernel(tc, h_inter, adjacency, Wd, eps, alpha, o
                         in_=h_view[c, u, :, :, HD * n : HD * (n + 1)],
                     )
 
-        def load_adjacency(k, halves=(0, 1)):
+        def load_adjacency(k, halves=(0, 1), split=False):
             c, n = units[k]
             if halves[0] == 0:
                 a_raw[k] = work.tile([P, PACK, S], BF16, name="a_raw", bufs=A_BUFS)
             for u in halves:
-                nc.sync.dma_start(
-                    out=a_raw[k][:, 2 * u : 2 * u + 2, :].rearrange("p e j -> p (e j)"), in_=a_view[n, c, :, u, :]
-                )
+                if split:
+                    for e in range(2):
+                        nc.sync.dma_start(out=a_raw[k][:, 2 * u + e, :], in_=a_view[n, c, :, u, S * e : S * (e + 1)])
+                else:
+                    nc.sync.dma_start(
+                        out=a_raw[k][:, 2 * u : 2 * u + 2, :].rearrange("p e j -> p (e j)"), in_=a_view[n, c, :, u, :]
+                    )
 
         def load_wd(n, half):
             cols = slice(D // 2 * half, D // 2 * (half + 1))
@@ -173,11 +176,12 @@ def tile_llamamlp_halfwaygin_pa_kernel(tc, h_inter, adjacency, Wd, eps, alpha, o
                     out=dst.rearrange("p (x i) t -> p x t i", i=4), in_=src.rearrange("p t (x i) -> p x t i", i=4)
                 )
 
-        def quantise_wd(q):
+        def quantise_wd(q, heads=range(HEADS)):
+            cols = slice(CHUNK * heads[0], CHUNK * (heads[-1] + 1))
             nc.vector.quantize_mx(
-                out=wd_codes[:, q, :].bitcast(FP8X4),
-                scales=wd_scales[:, q, :],
-                in_=wd_grouped[q][:].rearrange("p n x t -> p (n x t)"),
+                out=wd_codes[:, q, cols].bitcast(FP8X4),
+                scales=wd_scales[:, q, cols],
+                in_=wd_grouped[q][:, heads[0] : heads[-1] + 1, :, :].rearrange("p n x t -> p (n x t)"),
             )
 
         def transpose_adjacency(k, tiles, copies=(nc.scalar.copy,)):
@@ -252,12 +256,13 @@ def tile_llamamlp_halfwaygin_pa_kernel(tc, h_inter, adjacency, Wd, eps, alpha, o
                     op1=ALU.add,
                 )
 
-        def quantise_g(k):
+        def quantise_g(k, tiles):
             c, n = units[k]
+            cols = slice(P * tiles[0], P * (tiles[-1] + 1))
             nc.vector.quantize_mx(
-                out=g_codes[:, n, c, :].bitcast(FP8X4),
-                scales=g_scales[:, n, c, :],
-                in_=g_grouped[k][:].rearrange("p x t -> p (x t)"),
+                out=g_codes[:, n, c, cols].bitcast(FP8X4),
+                scales=g_scales[:, n, c, cols],
+                in_=g_grouped[k][:, cols, :].rearrange("p x t -> p (x t)"),
             )
 
         def project(q, c, copies, split=False):
@@ -287,11 +292,11 @@ def tile_llamamlp_halfwaygin_pa_kernel(tc, h_inter, adjacency, Wd, eps, alpha, o
         scopy = nc.scalar.copy
         last = len(units) - 1
         all_tiles = range(PACK)
+        wd_ready = {5: (0, 1), 6: (2,), 7: (3,)}
         h_parts = {0: [(1, 0), (1, 1)], 1: [(2, 0)], 2: [(2, 1)], 3: [(3, 0)], 4: [(3, 1)]};
 
-        load_h(0, (0,))
-        load_adjacency(0, (0,))
-        load_h(0, (1,))
+        load_adjacency(0, (0,), split=True)
+        load_h(0)
         load_adjacency(0, (1,))
         load_adjacency(1)
         load_h(1)
@@ -300,16 +305,17 @@ def tile_llamamlp_halfwaygin_pa_kernel(tc, h_inter, adjacency, Wd, eps, alpha, o
         load_adjacency(3)
         load_h(2, (1,))
 
-        keep_clock(6)
+        keep_clock(3)
+        transpose_adjacency(0, (0, 1))
+        quantise_adjacency(0, (0, 1))
+        nc.vector.tensor_scalar_add(out=one_plus_eps[:], in0=eps_bf[:], scalar1=1.0)
         transpose_h(0)
         regroup_h_vector(0, 0, 0)
         regroup_h_vector(0, 0, 1)
-        transpose_adjacency(0, (0, 1))
         nc.vector.tensor_copy(out=alpha_f[:], in_=alpha_bf[:])
-        quantise_h(0, 0)
-        quantise_adjacency(0, (0, 1))
         regroup_h_vector(0, 1, 0)
-        regroup_h_tensor(0, 1, 1)
+        regroup_h_vector(0, 1, 1)
+        quantise_h(0, 0)
         transpose_adjacency(0, (2, 3))
         quantise_h(0, 1)
         quantise_adjacency(0, (2, 3))
@@ -327,22 +333,23 @@ def tile_llamamlp_halfwaygin_pa_kernel(tc, h_inter, adjacency, Wd, eps, alpha, o
                 if k + A_BUFS == last:
                     for n in range(HEADS):
                         load_wd(n, 1)
-            for head, block in h_parts.get(k - 1, []):
-                quantise_h(head, block)
             for head, block in h_parts.get(k, []):
                 if k == 0:
                     continue
                 regroup_h_scalar(head, block, 1, slice(0, 1))
             if k in (3, 4):
                 regroup_wd(0, k - 3, "tensor")
+            if k in wd_ready:
+                quantise_wd(0, wd_ready[k])
             if k == last:
-                quantise_wd(0)
                 for n in range(3):
                     regroup_wd(1, n, "scalar")
-            if k > 0:
-                quantise_g(k - 1)
             if k < last:
                 quantise_adjacency(k + 1, all_tiles)
+            for head, block in h_parts.get(k - 1, []):
+                quantise_h(head, block)
+            if k > 0:
+                quantise_g(k - 1, all_tiles)
             if k > 0:
                 for head, block in h_parts.get(k, []):
                     regroup_h_gpsimd(head, block, 0)
@@ -354,13 +361,16 @@ def tile_llamamlp_halfwaygin_pa_kernel(tc, h_inter, adjacency, Wd, eps, alpha, o
             if k == 0:
                 regroup_h_gpsimd(1, 0, 0)
                 regroup_h_gpsimd(1, 0, 1, slice(0, 1), hold=False)
-            mix(k, all_tiles)
+            if k < last:
+                mix(k, all_tiles)
             if k == 0:
                 regroup_h_vector(1, 0, 1, slice(1, 2))
                 regroup_h_vector(1, 1, 0)
                 regroup_h_vector(1, 1, 1)
+        for tiles in ((0, 1), (2, 3)):
+            mix(last, tiles)
+            quantise_g(last, tiles)
         project(0, 0, (scopy, scopy))
-        quantise_g(last)
         quantise_wd(1)
         project(0, 1, (scopy, scopy))
 

from contextlib import ExitStack

import concourse.mybir as mybir
from concourse.masks import make_identity

F32 = mybir.dt.float32
BF16 = mybir.dt.bfloat16
U32 = mybir.dt.uint32
U8 = mybir.dt.uint8
FP8X4 = mybir.dt.float8_e4m3fn_x4
ALU = mybir.AluOpType
ACT = mybir.ActivationFunctionType

P = 128
PACK = 4
K_PASS = P * PACK
S = 1024
HEADS = 4
HD = 512
D = 1024
BLOCKS = S // K_PASS
CHUNK = 256
CHUNKS = D // CHUNK
A_BUFS = 4
GROUPED_BUFS = 3

FLOPS = 2 * HEADS * S * S * HD + 2 * S * HEADS * HD * D


def tile_llamamlp_halfwaygin_pa_kernel(tc, h_inter, adjacency, Wd, eps, alpha, out):
    nc = tc.nc

    h_view = h_inter.rearrange("b (c u p e) f -> (b c) u p e f", c=BLOCKS, u=2, p=P, e=2)
    a_view = adjacency.rearrange("b n (c u p e) j -> (b n) c p u (e j)", c=BLOCKS, u=2, p=P, e=2)
    wd_view = Wd.rearrange("(n u p e) d -> n u p e d", n=HEADS, u=2, p=P, e=2)
    out_view = out.rearrange("b (c u p e) d -> (b c) u p e d", c=BLOCKS, u=2, p=P, e=2)

    units = [(c, n) for n in range(HEADS) for c in range(BLOCKS)]

    with ExitStack() as ctx:
        keep = ctx.enter_context(tc.tile_pool(name="keep", bufs=1))
        work = ctx.enter_context(tc.tile_pool(name="work", bufs=2))
        psum = ctx.enter_context(tc.psum_pool(name="psum", bufs=8))
        ctx.enter_context(tc.manual_schedule())

        ident = keep.tile([P, P], F32, name="ident")
        make_identity(nc, ident[:])
        ident_bf = keep.tile([P, P], BF16, name="ident_bf")
        make_identity(nc, ident_bf[:])
        eps_bf = keep.tile([P, HEADS], BF16, name="eps_bf")
        alpha_bf = keep.tile([P, HEADS], BF16, name="alpha_bf")
        nc.scalar.dma_start(out=eps_bf[:], in_=eps.partition_broadcast(P))
        nc.scalar.dma_start(out=alpha_bf[:], in_=alpha.partition_broadcast(P))
        one_plus_eps = keep.tile([P, HEADS], F32, name="one_plus_eps")
        alpha_f = keep.tile([P, HEADS], F32, name="alpha_f")
        zeros = keep.tile([P, K_PASS], BF16, name="zeros")
        nc.vector.memset(zeros[:], 0.0)
        unused = keep.tile([P, 16], BF16, name="unused")
        nc.scalar.copy(out=unused[:], in_=zeros[:, 0:16])

        h_raw = [keep.tile([P, BLOCKS, PACK, HD], BF16, name="h_raw%d" % n) for n in range(HEADS)]
        wd_raw = [keep.tile([P, PACK, D], BF16, name="wd_raw%d" % n) for n in range(HEADS)]
        h_codes = keep.tile([P, HEADS, BLOCKS * HD], U32, name="h_codes", align_bytes=64)
        h_scales = keep.tile([P, HEADS, BLOCKS * HD], U8, name="h_scales", align_bytes=64)
        wd_codes = keep.tile([P, CHUNKS, HEADS * CHUNK], U32, name="wd_codes", align_bytes=64)
        wd_scales = keep.tile([P, CHUNKS, HEADS * CHUNK], U8, name="wd_scales", align_bytes=64)
        g_codes = keep.tile([P, HEADS, BLOCKS, K_PASS], U32, name="g_codes", align_bytes=64)
        g_scales = keep.tile([P, HEADS, BLOCKS, K_PASS], U8, name="g_scales", align_bytes=64)

        def keep_clock(passes):
            idle = psum.tile([P, K_PASS], F32, tag="bank")
            for i in range(passes):
                nc.tensor.matmul(idle[:], zeros[:, :P], zeros[:], start=True, stop=True)

        a_raw = {}
        a_grouped = {}
        a_codes = {}
        a_scales = {}
        h_grouped = {}
        h_scaled = {}
        g_grouped = {}
        wd_grouped = {}

        def load_h(n, blocks=range(BLOCKS)):
            for c in blocks:
                for u in range(2):
                    nc.sync.dma_start(
                        out=h_raw[n][:, c, 2 * u : 2 * u + 2, :],
                        in_=h_view[c, u, :, :, HD * n : HD * (n + 1)],
                    )

        def load_adjacency(k, halves=(0, 1), split=False):
            c, n = units[k]
            if halves[0] == 0:
                a_raw[k] = work.tile([P, PACK, S], BF16, name="a_raw", bufs=A_BUFS)
            for u in halves:
                if split:
                    for e in range(2):
                        nc.sync.dma_start(out=a_raw[k][:, 2 * u + e, :], in_=a_view[n, c, :, u, S * e : S * (e + 1)])
                else:
                    nc.sync.dma_start(
                        out=a_raw[k][:, 2 * u : 2 * u + 2, :].rearrange("p e j -> p (e j)"), in_=a_view[n, c, :, u, :]
                    )

        def load_wd(n, half):
            cols = slice(D // 2 * half, D // 2 * (half + 1))
            for u in range(2):
                nc.sync.dma_start(out=wd_raw[n][:, 2 * u : 2 * u + 2, cols], in_=wd_view[n, u, :, :, cols])

        def grouped_h(n, c, e):
            if n not in h_grouped:
                h_grouped[n] = work.tile(
                    [P, BLOCKS, HD, PACK], BF16, name="h_grouped", tag="grouped", bufs=GROUPED_BUFS, align_bytes=64
                )
            return h_grouped[n][:, c, :, :].rearrange("p (u e q) t -> p e u q t", u=2, e=2)[:, e, :, :, :]

        def features(n, c, e):
            return h_raw[n][:, c, :, :].rearrange("p t (u q e) -> p e u q t", u=2, e=2)[:, e, :, :, :]

        def regroup_h_vector(n, c, e, us=slice(0, 2)):
            nc.vector.tensor_copy(out=grouped_h(n, c, e)[:, us, :, :], in_=features(n, c, e)[:, us, :, :])

        def regroup_h_gpsimd(n, c, e, us=slice(0, 2), hold=True):
            dst = grouped_h(n, c, e)[:, us, :, :]
            src = features(n, c, e)[:, us, :, :]
            if hold:
                nc.vector.tensor_copy(out=dst[:, 0, 0:8, :], in_=src[:, 0, 0:8, :])
            nc.gpsimd.tensor_scalar(out=dst, in0=src, scalar1=1.0, scalar2=0.0, op0=ALU.mult, op1=ALU.add)

        def regroup_h_scalar(n, c, e, us):
            nc.scalar.copy(out=grouped_h(n, c, e)[:, us, :, :], in_=features(n, c, e)[:, us, :, :])

        def regroup_h_tensor(n, c, e, us=slice(0, 2)):
            dst = grouped_h(n, c, e)[:, us, :, :]
            src = features(n, c, e)[:, us, :, :]
            halves = us.stop - us.start
            turned = psum.tile([P, halves, P, PACK], BF16, tag="bank")
            for u in range(halves):
                nc.tensor.matmul(turned[:, u, :, :], ident_bf[:], src[:, u, :, :], start=True, stop=True)
            nc.scalar.copy(
                out=dst.rearrange("p u q t -> p u (q t)").bitcast(F32),
                in_=turned[:].rearrange("p u q t -> p u (q t)").bitcast(F32),
            )

        def quantise_h(n, c):
            cols = slice(HD * c, HD * (c + 1))
            nc.vector.quantize_mx(
                out=h_codes[:, n, cols].bitcast(FP8X4),
                scales=h_scales[:, n, cols],
                in_=h_grouped[n][:, c, :, :].rearrange("p x t -> p (x t)"),
            )

        def regroup_wd(q, n, way):
            if n == 0:
                wd_grouped[q] = work.tile(
                    [P, HEADS, CHUNK, PACK], BF16, name="wd_grouped", tag="grouped", bufs=GROUPED_BUFS, align_bytes=64
                )
            dst = wd_grouped[q][:, n, :, :]
            src = wd_raw[n][:, :, CHUNK * q : CHUNK * (q + 1)]
            if way == "gpsimd":
                src4 = src.rearrange("p t x -> p x t")
                nc.vector.tensor_copy(out=dst[:, 0:8, :], in_=src4[:, 0:8, :])
                nc.gpsimd.tensor_scalar(out=dst, in0=src4, scalar1=1.0, scalar2=0.0, op0=ALU.mult, op1=ALU.add)
            elif way == "tensor":
                turned = psum.tile([P, CHUNK, PACK], BF16, tag="bank")
                for x in range(0, CHUNK, P):
                    rows = src[:, :, x : x + P].rearrange("p t x -> p x t")
                    nc.tensor.matmul(turned[:, x : x + P, :], ident_bf[:], rows, start=True, stop=True)
                nc.scalar.copy(
                    out=dst.rearrange("p x t -> p (x t)").bitcast(F32),
                    in_=turned[:].rearrange("p x t -> p (x t)").bitcast(F32),
                )
            else:
                copy = nc.vector.tensor_copy if way == "vector" else nc.scalar.copy
                copy(
                    out=dst.rearrange("p (x i) t -> p x t i", i=4), in_=src.rearrange("p t (x i) -> p x t i", i=4)
                )

        def quantise_wd(q, heads=range(HEADS)):
            cols = slice(CHUNK * heads[0], CHUNK * (heads[-1] + 1))
            nc.vector.quantize_mx(
                out=wd_codes[:, q, cols].bitcast(FP8X4),
                scales=wd_scales[:, q, cols],
                in_=wd_grouped[q][:, heads[0] : heads[-1] + 1, :, :].rearrange("p n x t -> p (n x t)"),
            )

        def transpose_adjacency(k, tiles, copies=(nc.scalar.copy,)):
            for ti in tiles:
                a_words = a_raw[k][:, ti, :].bitcast(F32)
                at_ps = psum.tile([P, BLOCKS, 2, P], F32, tag="bank")
                for c in range(BLOCKS):
                    for u in range(2):
                        w0 = (2 * c + u) * P
                        nc.tensor.transpose(at_ps[:, c, u, :], a_words[:, w0 : w0 + P], ident[:])
                if ti % 2 == 0:
                    a_grouped[(k, ti // 2)] = work.tile([P, 2, BLOCKS, P, PACK], BF16, name="a_grouped", align_bytes=64)
                copy = copies[ti % len(copies)]
                copy(
                    out=a_grouped[(k, ti // 2)][:, ti % 2, :, :, :].bitcast(F32),
                    in_=at_ps[:].rearrange("p c u i -> p c i u"),
                )

        def quantise_adjacency(k, tiles, width=1):
            if tiles[0] == 0:
                a_codes[k] = work.tile([P, PACK, BLOCKS * P], U32, name="a_codes", align_bytes=64)
                a_scales[k] = work.tile([P, PACK, BLOCKS * P], U8, name="a_scales", align_bytes=64)
            for ti in range(tiles[0], tiles[-1] + 1, width):
                part = slice(ti % 2, ti % 2 + width)
                nc.vector.quantize_mx(
                    out=a_codes[k][:, ti : ti + width, :].rearrange("p t x -> p (t x)").bitcast(FP8X4),
                    scales=a_scales[k][:, ti : ti + width, :].rearrange("p t x -> p (t x)"),
                    in_=a_grouped[(k, ti // 2)][:, part, :, :, :].rearrange("p t c i e -> p (t c i e)"),
                )

        def transpose_h(k):
            c, n = units[k]
            h_scaled[k] = work.tile([P, PACK * P, PACK], F32, name="h_scaled")
            for pair in range(PACK // 2):
                ht_ps = psum.tile([P, 2, 2 * P], F32, tag="bank")
                for r in range(2):
                    h_words = h_raw[n][:, c, 2 * pair + r, :].bitcast(F32)
                    for u in range(2):
                        nc.tensor.transpose(ht_ps[:, u, P * r : P * (r + 1)], h_words[:, P * u : P * (u + 1)], ident[:])
                nc.scalar.activation(
                    out=h_scaled[k][:, 2 * P * pair : 2 * P * (pair + 1), :].rearrange("p x (u e) -> p x u e", e=2),
                    in_=ht_ps[:].bitcast(BF16).rearrange("p u (x e) -> p x u e", e=2),
                    func=ACT.Copy,
                    scale=one_plus_eps[:, n : n + 1],
                )

        def mix(k, tiles):
            c, n = units[k]
            if tiles[0] == 0:
                g_grouped[k] = work.tile([P, PACK * P, PACK], BF16, name="g_grouped", align_bytes=64)
            for ti in tiles:
                agg_ps = psum.tile([P, PACK, P], F32, tag="bank")
                for tf in range(PACK):
                    for cp in range(BLOCKS):
                        f_cols = slice(HD * cp + P * tf, HD * cp + P * (tf + 1))
                        i_cols = slice(P * cp, P * (cp + 1))
                        nc.tensor.matmul_mx(
                            out=agg_ps[:, tf, :],
                            lhsT=h_codes[:, n, f_cols].bitcast(FP8X4),
                            lhsT_scale=h_scales[:, n, f_cols],
                            rhs=a_codes[k][:, ti, i_cols].bitcast(FP8X4),
                            rhs_scale=a_scales[k][:, ti, i_cols],
                            start=(cp == 0),
                            stop=(cp == BLOCKS - 1),
                        )
                nc.vector.scalar_tensor_tensor(
                    out=g_grouped[k][:, P * ti : P * (ti + 1), :],
                    in0=agg_ps[:].rearrange("p t i -> p i t"),
                    scalar=alpha_f[:, n : n + 1],
                    in1=h_scaled[k][:, P * ti : P * (ti + 1), :],
                    op0=ALU.mult,
                    op1=ALU.add,
                )

        def quantise_g(k, tiles):
            c, n = units[k]
            cols = slice(P * tiles[0], P * (tiles[-1] + 1))
            nc.vector.quantize_mx(
                out=g_codes[:, n, c, cols].bitcast(FP8X4),
                scales=g_scales[:, n, c, cols],
                in_=g_grouped[k][:, cols, :].rearrange("p x t -> p (x t)"),
            )

        def project(q, c, copies, split=False):
            for u in range(2):
                for es in ((0,), (1,)) if split else ((0, 1),):
                    out_ps = psum.tile([P, len(es), CHUNK], F32, tag="bank")
                    for e in es:
                        i_cols = slice(P * (2 * u + e), P * (2 * u + e + 1))
                        for n in range(HEADS):
                            d_cols = slice(CHUNK * n, CHUNK * (n + 1))
                            nc.tensor.matmul_mx(
                                out=out_ps[:, e - es[0], :],
                                lhsT=g_codes[:, n, c, i_cols].bitcast(FP8X4),
                                lhsT_scale=g_scales[:, n, c, i_cols],
                                rhs=wd_codes[:, q, d_cols].bitcast(FP8X4),
                                rhs_scale=wd_scales[:, q, d_cols],
                                start=(n == 0),
                                stop=(n == HEADS - 1),
                            )
                    out_sb = work.tile([P, len(es), CHUNK], F32, name="out_sb", bufs=6)
                    copies[(u + es[0]) % 2](out=out_sb[:], in_=out_ps[:])
                    nc.sync.dma_start(
                        out=out_view[c, u, :, es[0] : es[-1] + 1, CHUNK * q : CHUNK * (q + 1)], in_=out_sb[:]
                    )

        vcopy = nc.vector.tensor_copy
        scopy = nc.scalar.copy
        last = len(units) - 1
        all_tiles = range(PACK)
        wd_ready = {5: (0, 1), 6: (2,), 7: (3,)}
        h_parts = {0: [(1, 0), (1, 1)], 1: [(2, 0)], 2: [(2, 1)], 3: [(3, 0)], 4: [(3, 1)]};

        load_adjacency(0, (0,), split=True)
        load_h(0)
        load_adjacency(0, (1,))
        load_adjacency(1)
        load_h(1)
        load_adjacency(2)
        load_h(2, (0,))
        load_adjacency(3)
        load_h(2, (1,))

        keep_clock(3)
        transpose_adjacency(0, (0, 1))
        quantise_adjacency(0, (0, 1))
        nc.vector.tensor_scalar_add(out=one_plus_eps[:], in0=eps_bf[:], scalar1=1.0)
        transpose_h(0)
        regroup_h_vector(0, 0, 0)
        regroup_h_vector(0, 0, 1)
        nc.vector.tensor_copy(out=alpha_f[:], in_=alpha_bf[:])
        regroup_h_vector(0, 1, 0)
        regroup_h_vector(0, 1, 1)
        quantise_h(0, 0)
        transpose_adjacency(0, (2, 3))
        quantise_h(0, 1)
        quantise_adjacency(0, (2, 3))
        keep_clock(2)

        for k in range(last + 1):
            if k < last:
                transpose_adjacency(k + 1, all_tiles)
                transpose_h(k + 1)
            if k + A_BUFS <= last:
                load_adjacency(k + A_BUFS)
                if k < BLOCKS:
                    load_h(3, (k,))
                load_wd(k, 0)
                if k + A_BUFS == last:
                    for n in range(HEADS):
                        load_wd(n, 1)
            for head, block in h_parts.get(k, []):
                if k == 0:
                    continue
                regroup_h_scalar(head, block, 1, slice(0, 1))
            if k in (3, 4):
                regroup_wd(0, k - 3, "tensor")
            if k in wd_ready:
                quantise_wd(0, wd_ready[k])
            if k == last:
                for n in range(3):
                    regroup_wd(1, n, "scalar")
            if k < last:
                quantise_adjacency(k + 1, all_tiles)
            for head, block in h_parts.get(k - 1, []):
                quantise_h(head, block)
            if k > 0:
                quantise_g(k - 1, all_tiles)
            if k > 0:
                for head, block in h_parts.get(k, []):
                    regroup_h_gpsimd(head, block, 0)
                    regroup_h_gpsimd(head, block, 1, slice(1, 2), hold=False)
            if k in (5, 6):
                regroup_wd(0, k - 3, "gpsimd")
            if k == last:
                regroup_wd(1, 3, "gpsimd")
            if k == 0:
                regroup_h_gpsimd(1, 0, 0)
                regroup_h_gpsimd(1, 0, 1, slice(0, 1), hold=False)
            if k < last:
                mix(k, all_tiles)
            if k == 0:
                regroup_h_vector(1, 0, 1, slice(1, 2))
                regroup_h_vector(1, 1, 0)
                regroup_h_vector(1, 1, 1)
        for tiles in ((0, 1), (2, 3)):
            mix(last, tiles)
            quantise_g(last, tiles)
        project(0, 0, (scopy, scopy))
        quantise_wd(1)
        project(0, 1, (scopy, scopy))

        for q in range(1, CHUNKS):
            if q + 1 < CHUNKS:
                for n in range(HEADS):
                    regroup_wd(q + 1, n, "scalar" if n == 0 else "vector")
                quantise_wd(q + 1)
            for c in range(BLOCKS):
                project(q, c, (scopy, vcopy if q == CHUNKS - 1 else scopy), split=(q == CHUNKS - 1 and c == BLOCKS - 1))
